import numpy as np
import ml_dtypes


def mxq(x, axis, fmt="e4m3"):
    dtype, down = {"e4m3": (ml_dtypes.float8_e4m3fn, 7), "e5m2": (ml_dtypes.float8_e5m2, 14)}[fmt]
    v = np.moveaxis(np.asarray(x, np.float32).astype(ml_dtypes.bfloat16).astype(np.float64), axis, -1)
    blocks = v.reshape(v.shape[:-1] + (-1, 32))
    amax = np.abs(blocks).max(-1, keepdims=True)
    byte = np.maximum(np.where(amax > 0, np.frexp(amax)[1] - 1 + 127, 0) - down, 1)
    scale = np.exp2(byte - 127.0)
    codes = (blocks / scale).astype(np.float32).astype(dtype).astype(np.float64)
    return np.moveaxis((codes * scale).reshape(v.shape), -1, axis)


WIDE = False


def mx_kscale(k):
    if not WIDE:
        return np.ones(k)
    levels = np.array([10, -10, 5, -5, 0])
    a = np.random.permutation(np.resize(levels, k // 512 * 4)).reshape(k // 512, 4)
    idx = np.arange(k)
    return np.exp2(a[idx // 512, idx % 128 // 32])


BF16 = ml_dtypes.bfloat16


def bf(x):
    return np.asarray(x, np.float32).astype(BF16)


def f64(x):
    return np.asarray(x).astype(np.float64)


E2M1 = np.array([0.0, 0.5, 1.0, 1.5, 2.0, 3.0, 4.0, 6.0, -0.0, -0.5, -1.0, -1.5, -2.0, -3.0, -4.0, -6.0])


def pack_weight(w, fmt):
    k, n = w.shape
    w = f64(bf(w)).reshape(k // 32, 32, n)
    amax = np.abs(w).max(1)
    if fmt == "e4m3":
        byte = np.frexp(amax)[1] - 1 + 127 - 7
    else:
        mant, ex = np.frexp(amax / 6.0)
        byte = np.where(mant > 0.5, ex, ex - 1) + 127
    byte = np.clip(np.where(amax > 0, byte, 1), 1, 254)
    scaled = (w * np.exp2(127.0 - byte)[:, None, :]).reshape(k, n).astype(np.float32)
    by_word = np.ascontiguousarray(scaled.reshape(k // 512, 128, 4, n).transpose(0, 1, 3, 2))
    if fmt == "e4m3":
        words = by_word.astype(ml_dtypes.float8_e4m3fn).view(np.uint8)
    else:
        c = by_word.astype(ml_dtypes.float4_e2m1fn).view(np.uint8) & 0xF
        words = c[..., 0::2] | (c[..., 1::2] << 4)
    return np.ascontiguousarray(words), np.ascontiguousarray(byte.astype(np.uint8).reshape(k // 512, 16, n))


def unpack_weight(words, scales, fmt):
    g, p, n, _ = words.shape
    if fmt == "e4m3":
        vals = np.ascontiguousarray(words).view(ml_dtypes.float8_e4m3fn).astype(np.float64)
    else:
        nib = np.empty((g, p, n, 4), np.uint8)
        nib[..., 0::2] = words & 0xF
        nib[..., 1::2] = words >> 4
        vals = E2M1[nib]
    vals = vals * np.repeat(np.exp2(scales.astype(np.float64) - 127.0), 8, axis=1)[..., None]
    return vals.transpose(0, 1, 3, 2).reshape(g * 512, n)

def pack4(w):
    words, scales = pack_weight(w, "e2m1")
    return words.reshape(words.shape[0], 128, -1), scales


def unpack4(words, scales):
    return unpack_weight(words.reshape(words.shape[0], 128, -1, 2), scales, "e2m1")


B, L, F, D, N = 128, 32, 512, 1024, 8192
TOP = 0.8 * np.sqrt(2.0 * np.log(L))


def elu(v):
    return np.where(v > 0.0, v, np.exp(np.minimum(v, 0.0)) - 1.0)


def setup_inputs():
    s = mx_kscale(F)
    x = bf(np.random.standard_normal((B, L, F)) * s)
    words, scales = pack4((np.random.standard_normal((D, F)) / np.sqrt(F) / s).T)
    conv_b = bf(np.random.standard_normal(D) * 2.0 - TOP)
    return {"x": x,
            "conv_w_words": words,
            "conv_w_scales": scales,
            "conv_b": conv_b}


def reference(x, conv_w_words, conv_w_scales, conv_b):
    z = (mxq(f64(x), 2, "e4m3") @ unpack4(conv_w_words, conv_w_scales)) + f64(conv_b)
    return elu(z).max(axis=1)

@@ -1,0 +1,140 @@
+from contextlib import ExitStack
+
+import concourse.mybir as mybir
+from concourse.masks import make_identity
+
+BF16 = mybir.dt.bfloat16
+F32 = mybir.dt.float32
+I32 = mybir.dt.int32
+U32 = mybir.dt.uint32
+U8 = mybir.dt.uint8
+FP8X4 = mybir.dt.float8_e4m3fn_x4
+FP4X4 = mybir.dt.float4_e2m1fn_x4
+EXP = mybir.ActivationFunctionType.Exp
+
+P = 128
+B, L, F, D = 128, 32, 512, 1024
+PACK = 4
+HALF = 512
+HALVES = D // HALF
+PAIR = 2
+PAIRS = L // PAIR
+WORDS = F // 2
+AHEAD = 2
+
+FLOPS = 2 * B * L * F * D
+
+
+def tile_conceptembedmodel_pa_kernel(tc, x, conv_w_words, conv_w_scales, conv_b, out):
+    nc = tc.nc
+    with ExitStack() as ctx:
+        const = ctx.enter_context(tc.tile_pool(name="const", bufs=1))
+        x_pool = ctx.enter_context(tc.tile_pool(name="x_pool", bufs=PAIRS))
+        stage = ctx.enter_context(tc.tile_pool(name="stage", bufs=AHEAD + 1))
+        tail = ctx.enter_context(tc.tile_pool(name="tail", bufs=HALVES))
+        psum_t = ctx.enter_context(tc.psum_pool(name="psum_t", bufs=2))
+        psum_z = ctx.enter_context(tc.psum_pool(name="psum_z", bufs=6))
+
+        w_scales = const.tile([P, D], U8, align_bytes=64)
+        nc.vector.memset(w_scales[:].bitcast(I32), 0)
+        zero_col = const.tile([P, 1], F32)
+        nc.vector.memset(zero_col[:], 0.0)
+        one_col = const.tile([P, 1], F32)
+        nc.scalar.activation(out=one_col[:], in_=zero_col[:], func=EXP)
+        ident = const.tile([P, P], F32)
+        make_identity(nc, ident[:])
+
+        x_pairs = []
+
+        def load_pair(j):
+            x_pair = x_pool.tile([P, PAIR * F], BF16, name="x_pair")
+            nc.sync.dma_start(
+                out=x_pair[:],
+                in_=x[:, PAIR * j : PAIR * (j + 1), :].rearrange("b l f -> b (l f)"),
+            )
+            x_pairs.append(x_pair)
+
+        load_pair(0)
+        scale_rows = conv_w_scales.rearrange("g q n -> (g q) n")
+        for quadrant in range(4):
+            nc.sync.dma_start(
+                out=w_scales[32 * quadrant : 32 * quadrant + 4, :].bitcast(I32),
+                in_=scale_rows[4 * quadrant : 4 * quadrant + 4, :].bitcast(I32),
+            )
+        w_words = const.tile([P, 2 * D], U8, align_bytes=64)
+        nc.sync.dma_start(
+            out=w_words[:].bitcast(I32),
+            in_=conv_w_words.rearrange("g p n -> (g p) n").bitcast(I32),
+        )
+        for j in range(1, PAIRS):
+            load_pair(j)
+        bias = const.tile([P, D], BF16)
+        nc.sync.dma_start(out=bias[:], in_=conv_b.partition_broadcast(P))
+
+        best = [const.tile([P, HALF], F32, name="best%d" % h) for h in range(HALVES)]
+        quantised = {}
+
+        def prepare(j):
+            x_words = x_pairs[j][:].bitcast(F32)
+            turned = psum_t.tile([P, PAIR, 2, B], F32)
+            for i in range(PAIR):
+                for u in range(2):
+                    nc.tensor.transpose(
+                        turned[:, i, u, :],
+                        x_words[:, WORDS * i + u : WORDS * (i + 1) : 2],
+                        ident[:],
+                    )
+            grouped = stage.tile([P, PAIR * B * PACK], BF16, align_bytes=64)
+            nc.scalar.copy(
+                out=grouped[:].bitcast(F32).rearrange("p (i b u) -> p i b u", i=PAIR, u=2),
+                in_=turned[:].rearrange("p i u b -> p i b u"),
+            )
+            codes = stage.tile([P, PAIR * B], U32, align_bytes=64)
+            scales = stage.tile([P, PAIR * B], U8, align_bytes=64)
+            nc.vector.quantize_mx(out=codes[:].bitcast(FP8X4), scales=scales[:], in_=grouped[:])
+            quantised[j] = (codes, scales)
+
+        def multiply(j):
+            codes, scales = quantised[j]
+            for i in range(PAIR):
+                rows = slice(B * i, B * (i + 1))
+                for h in range(HALVES):
+                    z = psum_z.tile([P, HALF], F32)
+                    nc.tensor.matmul_mx(
+                        out=z[:],
+                        lhsT=codes[:, rows].bitcast(FP8X4),
+                        lhsT_scale=scales[:, rows],
+                        rhs=w_words[:, 2 * HALF * h : 2 * HALF * (h + 1)].bitcast(FP4X4),
+                        rhs_scale=w_scales[:, HALF * h : HALF * (h + 1)],
+                        start=True,
+                        stop=True,
+                    )
+                    if j == 0 and i == 0:
+                        nc.scalar.copy(out=best[h][:], in_=z[:])
+                    else:
+                        nc.vector.tensor_max(out=best[h][:], in0=z[:], in1=best[h][:])
+
+        for j in range(PAIRS + AHEAD):
+            if j < PAIRS:
+                prepare(j)
+            if j >= AHEAD:
+                multiply(j - AHEAD)
+
+        for h in range(HALVES):
+            cols = slice(HALF * h, HALF * (h + 1))
+            v = tail.tile([P, HALF], F32)
+            nc.vector.tensor_add(out=v[:], in0=best[h][:], in1=bias[:, cols])
+            low = tail.tile([P, HALF], F32)
+            nc.vector.tensor_scalar_min(out=low[:], in0=v[:], scalar1=0.0)
+            grown = tail.tile([P, HALF], F32)
+            nc.scalar.activation(out=grown[:], in_=low[:], func=EXP)
+            result = tail.tile([P, HALF], F32)
+            nc.vector.scalar_tensor_tensor(
+                out=result[:],
+                in0=grown[:],
+                scalar=-1.0,
+                in1=v[:],
+                op0=mybir.AluOpType.add,
+                op1=mybir.AluOpType.max,
+            )
+            nc.sync.dma_start(out=out[:, cols], in_=result[:])

@@ -11,6 +11,7 @@ U8 = mybir.dt.uint8
 FP8X4 = mybir.dt.float8_e4m3fn_x4
 FP4X4 = mybir.dt.float4_e2m1fn_x4
 EXP = mybir.ActivationFunctionType.Exp
+RELU = mybir.ActivationFunctionType.Relu
 
 P = 128
 B, L, F, D = 128, 32, 512, 1024
@@ -20,7 +21,8 @@ HALVES = D // HALF
 PAIR = 2
 PAIRS = L // PAIR
 WORDS = F // 2
-AHEAD = 2
+FRONT = 2
+GP_PAIRS = 2
 
 FLOPS = 2 * B * L * F * D
 
@@ -30,7 +32,10 @@ def tile_conceptembedmodel_pa_kernel(tc, x, conv_w_words, conv_w_scales, conv_b,
     with ExitStack() as ctx:
         const = ctx.enter_context(tc.tile_pool(name="const", bufs=1))
         x_pool = ctx.enter_context(tc.tile_pool(name="x_pool", bufs=PAIRS))
-        stage = ctx.enter_context(tc.tile_pool(name="stage", bufs=AHEAD + 1))
+        stage = ctx.enter_context(tc.tile_pool(name="stage", bufs=3))
+        keep = ctx.enter_context(tc.tile_pool(name="keep", bufs=PAIRS))
+        parked_pool = ctx.enter_context(tc.tile_pool(name="parked_pool", bufs=PAIR * GP_PAIRS * HALVES))
+        gp_pool = ctx.enter_context(tc.tile_pool(name="gp_pool", bufs=2 * HALVES))
         tail = ctx.enter_context(tc.tile_pool(name="tail", bufs=HALVES))
         psum_t = ctx.enter_context(tc.psum_pool(name="psum_t", bufs=2))
         psum_z = ctx.enter_context(tc.psum_pool(name="psum_z", bufs=6))
@@ -89,36 +94,77 @@ def tile_conceptembedmodel_pa_kernel(tc, x, conv_w_words, conv_w_scales, conv_b,
                 out=grouped[:].bitcast(F32).rearrange("p (i b u) -> p i b u", i=PAIR, u=2),
                 in_=turned[:].rearrange("p i u b -> p i b u"),
             )
-            codes = stage.tile([P, PAIR * B], U32, align_bytes=64)
-            scales = stage.tile([P, PAIR * B], U8, align_bytes=64)
+            codes = keep.tile([P, PAIR * B], U32, align_bytes=64)
+            scales = keep.tile([P, PAIR * B], U8, align_bytes=64)
             nc.vector.quantize_mx(out=codes[:].bitcast(FP8X4), scales=scales[:], in_=grouped[:])
             quantised[j] = (codes, scales)
 
-        def multiply(j):
+        def product(j, i, h):
             codes, scales = quantised[j]
+            rows = slice(B * i, B * (i + 1))
+            z = psum_z.tile([P, HALF], F32)
+            nc.tensor.matmul_mx(
+                out=z[:],
+                lhsT=codes[:, rows].bitcast(FP8X4),
+                lhsT_scale=scales[:, rows],
+                rhs=w_words[:, 2 * HALF * h : 2 * HALF * (h + 1)].bitcast(FP4X4),
+                rhs_scale=w_scales[:, HALF * h : HALF * (h + 1)],
+                start=True,
+                stop=True,
+            )
+            return z
+
+        def fold_on_vector(j):
             for i in range(PAIR):
-                rows = slice(B * i, B * (i + 1))
                 for h in range(HALVES):
-                    z = psum_z.tile([P, HALF], F32)
-                    nc.tensor.matmul_mx(
-                        out=z[:],
-                        lhsT=codes[:, rows].bitcast(FP8X4),
-                        lhsT_scale=scales[:, rows],
-                        rhs=w_words[:, 2 * HALF * h : 2 * HALF * (h + 1)].bitcast(FP4X4),
-                        rhs_scale=w_scales[:, HALF * h : HALF * (h + 1)],
-                        start=True,
-                        stop=True,
-                    )
+                    z = product(j, i, h)
                     if j == 0 and i == 0:
                         nc.scalar.copy(out=best[h][:], in_=z[:])
                     else:
                         nc.vector.tensor_max(out=best[h][:], in0=z[:], in1=best[h][:])
 
-        for j in range(PAIRS + AHEAD):
-            if j < PAIRS:
+        parked = []
+
+        def park(j):
+            for i in range(PAIR):
+                halves = []
+                for h in range(HALVES):
+                    z = product(j, i, h)
+                    z_sb = parked_pool.tile([P, HALF], F32, name="z_sb")
+                    nc.scalar.copy(out=z_sb[:], in_=z[:])
+                    halves.append(z_sb)
+                parked.append(halves)
+
+        def fold_on_gpsimd(side, fresh):
+            rises = []
+            for h in range(HALVES):
+                rise = gp_pool.tile([P, HALF], F32, name="rise")
+                nc.gpsimd.tensor_sub(out=rise[:], in0=fresh[h][:], in1=side[h][:])
+                rises.append(rise)
+            for h in range(HALVES):
+                nc.scalar.activation(out=rises[h][:], in_=rises[h][:], func=RELU)
+            for h in range(HALVES):
+                nc.gpsimd.tensor_add(out=side[h][:], in0=side[h][:], in1=rises[h][:])
+
+        with tc.manual_schedule():
+            folded = 0
+            for j in range(FRONT):
                 prepare(j)
-            if j >= AHEAD:
-                multiply(j - AHEAD)
+            for first in range(FRONT, PAIRS, FRONT):
+                fold_on_vector(folded)
+                folded += 1
+                for j in range(first, first + FRONT):
+                    prepare(j)
+            for j in range(PAIRS - GP_PAIRS, PAIRS):
+                fold_on_vector(folded)
+                folded += 1
+                park(j)
+            for fresh in parked[1:]:
+                fold_on_gpsimd(parked[0], fresh)
+            for j in range(folded, PAIRS - GP_PAIRS):
+                fold_on_vector(j)
+            for h in range(HALVES):
+                nc.vector.tensor_max(out=best[h][:], in0=parked[0][h][:], in1=best[h][:])
 
         for h in range(HALVES):
             cols = slice(HALF * h, HALF * (h + 1))

@@ -22,7 +22,7 @@ PAIR = 2
 PAIRS = L // PAIR
 WORDS = F // 2
 FRONT = 2
-GP_PAIRS = 2
+GP_POSITIONS = 3
 
 FLOPS = 2 * B * L * F * D
 
@@ -34,7 +34,7 @@ def tile_conceptembedmodel_pa_kernel(tc, x, conv_w_words, conv_w_scales, conv_b,
         x_pool = ctx.enter_context(tc.tile_pool(name="x_pool", bufs=PAIRS))
         stage = ctx.enter_context(tc.tile_pool(name="stage", bufs=3))
         keep = ctx.enter_context(tc.tile_pool(name="keep", bufs=PAIRS))
-        parked_pool = ctx.enter_context(tc.tile_pool(name="parked_pool", bufs=PAIR * GP_PAIRS * HALVES))
+        parked_pool = ctx.enter_context(tc.tile_pool(name="parked_pool", bufs=GP_POSITIONS * HALVES))
         gp_pool = ctx.enter_context(tc.tile_pool(name="gp_pool", bufs=2 * HALVES))
         tail = ctx.enter_context(tc.tile_pool(name="tail", bufs=HALVES))
         psum_t = ctx.enter_context(tc.psum_pool(name="psum_t", bufs=2))
@@ -99,9 +99,9 @@ def tile_conceptembedmodel_pa_kernel(tc, x, conv_w_words, conv_w_scales, conv_b,
             nc.vector.quantize_mx(out=codes[:].bitcast(FP8X4), scales=scales[:], in_=grouped[:])
             quantised[j] = (codes, scales)
 
-        def product(j, i, h):
-            codes, scales = quantised[j]
-            rows = slice(B * i, B * (i + 1))
+        def product(l, h):
+            codes, scales = quantised[l // PAIR]
+            rows = slice(B * (l % PAIR), B * (l % PAIR + 1))
             z = psum_z.tile([P, HALF], F32)
             nc.tensor.matmul_mx(
                 out=z[:],
@@ -114,26 +114,22 @@ def tile_conceptembedmodel_pa_kernel(tc, x, conv_w_words, conv_w_scales, conv_b,
             )
             return z
 
-        def fold_on_vector(j):
-            for i in range(PAIR):
-                for h in range(HALVES):
-                    z = product(j, i, h)
-                    if j == 0 and i == 0:
-                        nc.scalar.copy(out=best[h][:], in_=z[:])
-                    else:
-                        nc.vector.tensor_max(out=best[h][:], in0=z[:], in1=best[h][:])
+        def fold_on_vector(l):
+            for h in range(HALVES):
+                z = product(l, h)
+                if l == 0:
+                    nc.scalar.copy(out=best[h][:], in_=z[:])
+                else:
+                    nc.vector.tensor_max(out=best[h][:], in0=z[:], in1=best[h][:])
 
-        parked = []
-
-        def park(j):
-            for i in range(PAIR):
-                halves = []
-                for h in range(HALVES):
-                    z = product(j, i, h)
-                    z_sb = parked_pool.tile([P, HALF], F32, name="z_sb")
-                    nc.scalar.copy(out=z_sb[:], in_=z[:])
-                    halves.append(z_sb)
-                parked.append(halves)
+        def park(l):
+            halves = []
+            for h in range(HALVES):
+                z = product(l, h)
+                z_sb = parked_pool.tile([P, HALF], F32, name="z_sb")
+                nc.scalar.copy(out=z_sb[:], in_=z[:])
+                halves.append(z_sb)
+            return halves
 
         def fold_on_gpsimd(side, fresh):
             rises = []
@@ -147,40 +143,47 @@ def tile_conceptembedmodel_pa_kernel(tc, x, conv_w_words, conv_w_scales, conv_b,
                 nc.gpsimd.tensor_add(out=side[h][:], in0=side[h][:], in1=rises[h][:])
 
         with tc.manual_schedule():
-            folded = 0
             for j in range(FRONT):
                 prepare(j)
+            folded = 0
             for first in range(FRONT, PAIRS, FRONT):
-                fold_on_vector(folded)
-                folded += 1
+                for l in range(folded, folded + PAIR):
+                    fold_on_vector(l)
+                folded += PAIR
                 for j in range(first, first + FRONT):
                     prepare(j)
-            for j in range(PAIRS - GP_PAIRS, PAIRS):
-                fold_on_vector(folded)
-                folded += 1
-                park(j)
+            parked = []
+            for gp_l in range(L - GP_POSITIONS, L):
+                for l in range(folded, folded + PAIR):
+                    fold_on_vector(l)
+                folded += PAIR
+                parked.append(park(gp_l))
             for fresh in parked[1:]:
                 fold_on_gpsimd(parked[0], fresh)
-            for j in range(folded, PAIRS - GP_PAIRS):
-                fold_on_vector(j)
+            for l in range(folded, L - GP_POSITIONS):
+                fold_on_vector(l)
             for h in range(HALVES):
                 nc.vector.tensor_max(out=best[h][:], in0=parked[0][h][:], in1=best[h][:])
 
-        for h in range(HALVES):
-            cols = slice(HALF * h, HALF * (h + 1))
-            v = tail.tile([P, HALF], F32)
-            nc.vector.tensor_add(out=v[:], in0=best[h][:], in1=bias[:, cols])
-            low = tail.tile([P, HALF], F32)
-            nc.vector.tensor_scalar_min(out=low[:], in0=v[:], scalar1=0.0)
-            grown = tail.tile([P, HALF], F32)
-            nc.scalar.activation(out=grown[:], in_=low[:], func=EXP)
-            result = tail.tile([P, HALF], F32)
-            nc.vector.scalar_tensor_tensor(
-                out=result[:],
-                in0=grown[:],
-                scalar=-1.0,
-                in1=v[:],
-                op0=mybir.AluOpType.add,
-                op1=mybir.AluOpType.max,
-            )
-            nc.sync.dma_start(out=out[:, cols], in_=result[:])
+            shifted = []
+            grown = []
+            for h in range(HALVES):
+                v = tail.tile([P, HALF], F32, name="v")
+                nc.vector.tensor_add(out=v[:], in0=best[h][:], in1=bias[:, HALF * h : HALF * (h + 1)])
+                low = tail.tile([P, HALF], F32, name="low")
+                nc.vector.tensor_scalar_min(out=low[:], in0=v[:], scalar1=0.0)
+                e = tail.tile([P, HALF], F32, name="e")
+                nc.scalar.activation(out=e[:], in_=low[:], func=EXP)
+                shifted.append(v)
+                grown.append(e)
+            for h in range(HALVES):
+                result = tail.tile([P, HALF], F32, name="result")
+                nc.vector.scalar_tensor_tensor(
+                    out=result[:],
+                    in0=grown[h][:],
+                    scalar=-1.0,
+                    in1=shifted[h][:],
+                    op0=mybir.AluOpType.add,
+                    op1=mybir.AluOpType.max,
+                )
+                nc.sync.dma_start(out=out[:, HALF * h : HALF * (h + 1)], in_=result[:])

@@ -12,17 +12,26 @@ FP8X4 = mybir.dt.float8_e4m3fn_x4
 FP4X4 = mybir.dt.float4_e2m1fn_x4
 EXP = mybir.ActivationFunctionType.Exp
 RELU = mybir.ActivationFunctionType.Relu
+IDENTITY = mybir.ActivationFunctionType.Identity
+MULT = mybir.AluOpType.mult
+ADD = mybir.AluOpType.add
+MAX = mybir.AluOpType.max
+MIN = mybir.AluOpType.min
 
 P = 128
 B, L, F, D = 128, 32, 512, 1024
-PACK = 4
-HALF = 512
-HALVES = D // HALF
-PAIR = 2
-PAIRS = L // PAIR
+D_TILES = D // P
+COLS = 512
+SLOTS = 4
 WORDS = F // 2
-FRONT = 2
-GP_POSITIONS = 3
+
+PLAN = "DPPDDD"
+OFFSET = 9
+LEAD = {"quant": 4, "negate": 4, "direct": 2, "pair": 9}
+FINISH_GROUPS = ((0, 4), (4, 7), (7, 8))
+BIAS_LAG = 1
+BACK_LAG = 8
+LAST_LAG = 6
 
 FLOPS = 2 * B * L * F * D
 
@@ -31,14 +40,15 @@ def tile_conceptembedmodel_pa_kernel(tc, x, conv_w_words, conv_w_scales, conv_b,
     nc = tc.nc
     with ExitStack() as ctx:
         const = ctx.enter_context(tc.tile_pool(name="const", bufs=1))
-        x_pool = ctx.enter_context(tc.tile_pool(name="x_pool", bufs=PAIRS))
-        stage = ctx.enter_context(tc.tile_pool(name="stage", bufs=3))
-        keep = ctx.enter_context(tc.tile_pool(name="keep", bufs=PAIRS))
-        parked_pool = ctx.enter_context(tc.tile_pool(name="parked_pool", bufs=GP_POSITIONS * HALVES))
-        gp_pool = ctx.enter_context(tc.tile_pool(name="gp_pool", bufs=2 * HALVES))
-        tail = ctx.enter_context(tc.tile_pool(name="tail", bufs=HALVES))
+        x_pool = ctx.enter_context(tc.tile_pool(name="x_pool", bufs=16))
+        stage = ctx.enter_context(tc.tile_pool(name="stage", bufs=8))
+        keep = ctx.enter_context(tc.tile_pool(name="keep", bufs=12))
+        sums = ctx.enter_context(tc.tile_pool(name="sums", bufs=8))
+        rises = ctx.enter_context(tc.tile_pool(name="rises", bufs=6))
+        fin = ctx.enter_context(tc.tile_pool(name="fin", bufs=3))
         psum_t = ctx.enter_context(tc.psum_pool(name="psum_t", bufs=2))
-        psum_z = ctx.enter_context(tc.psum_pool(name="psum_z", bufs=6))
+        psum_v = ctx.enter_context(tc.psum_pool(name="psum_v", bufs=3))
+        psum_s = ctx.enter_context(tc.psum_pool(name="psum_s", bufs=3))
 
         w_scales = const.tile([P, D], U8, align_bytes=64)
         nc.vector.memset(w_scales[:].bitcast(I32), 0)
@@ -48,18 +58,38 @@ def tile_conceptembedmodel_pa_kernel(tc, x, conv_w_words, conv_w_scales, conv_b,
         nc.scalar.activation(out=one_col[:], in_=zero_col[:], func=EXP)
         ident = const.tile([P, P], F32)
         make_identity(nc, ident[:])
+        ident_bf = const.tile([P, P], BF16)
+        make_identity(nc, ident_bf[:])
+        bias_rows = const.tile([P, P], BF16)
+        nc.gpsimd.memset(bias_rows[:], 0.0)
 
-        x_pairs = []
+        rows = x.rearrange("b l f -> (b l) f")
+        groups = []
+        blocks = []
+        b0 = 0
+        for kind in PLAN:
+            width = 16 if kind == "D" else 32
+            n_blocks = 1 if kind == "D" else 2
+            view = rows[L * b0 : L * (b0 + width), :].rearrange("(p n) f -> p (n f)", n=SLOTS * n_blocks)
+            group = {"kind": kind, "b0": b0, "width": width, "blocks": []}
+            for a in range(n_blocks):
+                group["blocks"].append(len(blocks))
+                blocks.append({
+                    "view": view[:, SLOTS * F * a : SLOTS * F * (a + 1)],
+                    "negated": kind == "P" and a == 0,
+                })
+            groups.append(group)
+            b0 += width
+        assert b0 == B
 
-        def load_pair(j):
-            x_pair = x_pool.tile([P, PAIR * F], BF16, name="x_pair")
-            nc.sync.dma_start(
-                out=x_pair[:],
-                in_=x[:, PAIR * j : PAIR * (j + 1), :].rearrange("b l f -> b (l f)"),
-            )
-            x_pairs.append(x_pair)
+        def load_tile(block, k):
+            x_tile = x_pool.tile([P, 2 * F], BF16, name="x_tile")
+            nc.sync.dma_start(out=x_tile[:], in_=block["view"][:, 2 * F * k : 2 * F * (k + 1)])
+            block["x"].append(x_tile)
 
-        load_pair(0)
+        for block in blocks:
+            block["x"] = []
+        load_tile(blocks[0], 0)
         scale_rows = conv_w_scales.rearrange("g q n -> (g q) n")
         for quadrant in range(4):
             nc.sync.dma_start(
@@ -71,119 +101,205 @@ def tile_conceptembedmodel_pa_kernel(tc, x, conv_w_words, conv_w_scales, conv_b,
             out=w_words[:].bitcast(I32),
             in_=conv_w_words.rearrange("g p n -> (g p) n").bitcast(I32),
         )
-        for j in range(1, PAIRS):
-            load_pair(j)
-        bias = const.tile([P, D], BF16)
-        nc.sync.dma_start(out=bias[:], in_=conv_b.partition_broadcast(P))
+        load_tile(blocks[0], 1)
+        for block in blocks[1:]:
+            load_tile(block, 0)
+            load_tile(block, 1)
+        nc.sync.dma_start(out=bias_rows[0:D_TILES, :], in_=conv_b.rearrange("(t p) -> t p", p=P))
 
-        best = [const.tile([P, HALF], F32, name="best%d" % h) for h in range(HALVES)]
-        quantised = {}
+        best = [const.tile([P, B], F32, name="best%d" % t) for t in range(D_TILES)]
+        bias_cols = const.tile([P, D_TILES], F32)
 
-        def prepare(j):
-            x_words = x_pairs[j][:].bitcast(F32)
-            turned = psum_t.tile([P, PAIR, 2, B], F32)
-            for i in range(PAIR):
-                for u in range(2):
-                    nc.tensor.transpose(
-                        turned[:, i, u, :],
-                        x_words[:, WORDS * i + u : WORDS * (i + 1) : 2],
-                        ident[:],
-                    )
-            grouped = stage.tile([P, PAIR * B * PACK], BF16, align_bytes=64)
-            nc.scalar.copy(
-                out=grouped[:].bitcast(F32).rearrange("p (i b u) -> p i b u", i=PAIR, u=2),
-                in_=turned[:].rearrange("p i u b -> p i b u"),
-            )
-            codes = keep.tile([P, PAIR * B], U32, align_bytes=64)
-            scales = keep.tile([P, PAIR * B], U8, align_bytes=64)
-            nc.vector.quantize_mx(out=codes[:].bitcast(FP8X4), scales=scales[:], in_=grouped[:])
-            quantised[j] = (codes, scales)
+        def turn(j):
+            block = blocks[j]
+            grouped = stage.tile([P, SLOTS * P * 4], BF16, align_bytes=64, name="grouped")
+            block["grouped"] = grouped
+            for k in range(2):
+                x_words = block["x"][k][:].bitcast(F32)
+                if (2 * j + k) % 5 in (0, 2):
+                    turned = psum_t.tile([P, 2, 2, P], F32, name="turned")
+                else:
+                    turned = psum_s.tile([P, 2, 2, P], F32, name="zs")
+                for i in range(2):
+                    for u in range(2):
+                        nc.tensor.transpose(
+                            turned[:, i, u, :],
+                            x_words[:, WORDS * i + u : WORDS * (i + 1) : 2],
+                            ident[:],
+                        )
+                nc.scalar.copy(
+                    out=grouped[:, 2 * F * k : 2 * F * (k + 1)].bitcast(F32).rearrange("p (i c u) -> p i c u", i=2, u=2),
+                    in_=turned[:].rearrange("p i u c -> p i c u"),
+                )
 
-        def product(l, h):
-            codes, scales = quantised[l // PAIR]
-            rows = slice(B * (l % PAIR), B * (l % PAIR + 1))
-            z = psum_z.tile([P, HALF], F32)
+        def quantise(source):
+            codes = keep.tile([P, COLS], U32, align_bytes=64, name="codes")
+            scales = keep.tile([P, COLS], U8, align_bytes=64, name="scales")
+            nc.vector.quantize_mx(out=codes[:].bitcast(FP8X4), scales=scales[:], in_=source[:])
+            return (codes, scales)
+
+        def negate(j):
+            block = blocks[j]
+            minus = stage.tile([P, SLOTS * P * 4], BF16, align_bytes=64, name="minus")
+            nc.vector.tensor_scalar_mul(out=minus[:], in0=block["grouped"][:], scalar1=-1.0)
+            block["grouped"] = minus
+
+        def multiply(z, t, operand, start, stop):
+            codes, scales = operand
             nc.tensor.matmul_mx(
                 out=z[:],
-                lhsT=codes[:, rows].bitcast(FP8X4),
-                lhsT_scale=scales[:, rows],
-                rhs=w_words[:, 2 * HALF * h : 2 * HALF * (h + 1)].bitcast(FP4X4),
-                rhs_scale=w_scales[:, HALF * h : HALF * (h + 1)],
-                start=True,
-                stop=True,
+                lhsT=w_words[:, 2 * P * t : 2 * P * (t + 1)].bitcast(FP4X4),
+                lhsT_scale=w_scales[:, P * t : P * (t + 1)],
+                rhs=codes[:].bitcast(FP8X4),
+                rhs_scale=scales[:],
+                start=start,
+                stop=stop,
             )
-            return z
 
-        def fold_on_vector(l):
-            for h in range(HALVES):
-                z = product(l, h)
-                if l == 0:
-                    nc.scalar.copy(out=best[h][:], in_=z[:])
-                else:
-                    nc.vector.tensor_max(out=best[h][:], in0=z[:], in1=best[h][:])
+        def fold(source, group, t):
+            nc.vector.tensor_reduce(
+                out=best[t][:, group["b0"] : group["b0"] + group["width"]],
+                in_=source[:].rearrange("p (i c q) -> p c i q", i=SLOTS, c=group["width"]),
+                axis=mybir.AxisListType.XY,
+                op=MAX,
+            )
 
-        def park(l):
-            halves = []
-            for h in range(HALVES):
-                z = product(l, h)
-                z_sb = parked_pool.tile([P, HALF], F32, name="z_sb")
-                nc.scalar.copy(out=z_sb[:], in_=z[:])
-                halves.append(z_sb)
-            return halves
+        made = {}
 
-        def fold_on_gpsimd(side, fresh):
-            rises = []
-            for h in range(HALVES):
-                rise = gp_pool.tile([P, HALF], F32, name="rise")
-                nc.gpsimd.tensor_sub(out=rise[:], in0=fresh[h][:], in1=side[h][:])
-                rises.append(rise)
-            for h in range(HALVES):
-                nc.scalar.activation(out=rises[h][:], in_=rises[h][:], func=RELU)
-            for h in range(HALVES):
-                nc.gpsimd.tensor_add(out=side[h][:], in0=side[h][:], in1=rises[h][:])
+        def produce(item):
+            kind = item[0]
+            if kind == "negate" or (kind == "quant" and not blocks[item[1]]["negated"]):
+                turn(item[1])
+            elif kind == "direct":
+                group, t = groups[item[1]], item[2]
+                z = psum_v.tile([P, COLS], F32, name="z")
+                multiply(z, t, blocks[group["blocks"][0]]["codes"], True, True)
+                made[item] = z
+            elif kind == "pair":
+                group, t = groups[item[1]], item[2]
+                first, second = blocks[group["blocks"][0]], blocks[group["blocks"][1]]
+                z_first = psum_s.tile([P, COLS], F32, name="zs")
+                multiply(z_first, t, first["codes"], True, True)
+                z_rise = psum_s.tile([P, COLS], F32, name="zs")
+                multiply(z_rise, t, second["codes"], True, False)
+                multiply(z_rise, t, first["codes"], False, True)
+                total = sums.tile([P, COLS], F32, name="total")
+                nc.scalar.copy(out=total[:], in_=z_first[:])
+                rise = rises.tile([P, COLS], F32, name="rise")
+                nc.scalar.activation(out=rise[:], in_=z_rise[:], func=RELU)
+                nc.gpsimd.tensor_sub(out=total[:], in0=rise[:], in1=total[:])
+                made[item] = total
+
+        def consume(item):
+            kind = item[0]
+            if kind == "quant":
+                blocks[item[1]]["codes"] = quantise(blocks[item[1]]["grouped"])
+            elif kind == "negate":
+                negate(item[1])
+            else:
+                fold(made[item], groups[item[1]], item[2])
+
+        def needs(item):
+            kind = item[0]
+            if kind == "direct":
+                return [("quant", groups[item[1]]["blocks"][0])]
+            if kind == "pair":
+                first, second = groups[item[1]]["blocks"]
+                return [("quant", first), ("quant", second)]
+            return []
+
+        shifted = {}
+        turned_back = {}
+        below = {}
+
+        def add_bias(t):
+            v = fin.tile([P, B], F32, name="v")
+            nc.scalar.activation(out=v[:], in_=best[t][:], func=IDENTITY, bias=bias_cols[:, t : t + 1])
+            shifted[t] = v
+
+        def turn_back(t):
+            t0, t1 = [g for g in FINISH_GROUPS if g[0] <= t < g[1]][0]
+            if t == t0:
+                back = psum_t.tile([P, COLS], F32, name="turned")
+                turned_back[t0] = back
+            back = turned_back[t0]
+            nc.tensor.transpose(back[:, P * (t - t0) : P * (t - t0 + 1)], shifted[t][:], ident[:])
+            if t == t1 - 1:
+                width = P * (t1 - t0)
+                grown = fin.tile([P, COLS], F32, name="grown")
+                nc.scalar.activation(out=grown[:, 0:width], in_=back[:, 0:width], func=EXP)
+                nc.scalar.activation(out=grown[:, 0:width], in_=grown[:, 0:width], func=RELU, bias=1.0, scale=-1.0)
+                below[t0] = grown
+
+        def store(t0, t1):
+            width = P * (t1 - t0)
+            final = fin.tile([P, COLS], F32, name="final")
+            nc.vector.scalar_tensor_tensor(
+                out=final[:, 0:width], in0=below[t0][:, 0:width], scalar=-1.0, in1=turned_back[t0][:, 0:width], op0=MULT, op1=MAX
+            )
+            nc.sync.dma_start(out=out[:, P * t0 : P * t1], in_=final[:, 0:width])
+
+        direct_groups = [g for g in range(len(groups)) if groups[g]["kind"] == "D"]
+        pair_groups = [g for g in range(len(groups)) if groups[g]["kind"] == "P"]
+        order = []
+        filled = 0
+        for j in range(len(blocks)):
+            steps = [("negate", j), ("quant", j)] if blocks[j]["negated"] else [("quant", j)]
+            for step in steps:
+                if step != steps[0] and filled < D_TILES:
+                    order.append(("direct", direct_groups[0], filled))
+                    filled += 1
+                order.append(step)
+            if j == 0:
+                order.append(("direct", direct_groups[0], filled))
+                filled += 1
+        straight = [("direct", g, t) for t in range(D_TILES) for g in direct_groups if ("direct", g, t) not in order]
+        paired = [("pair", g, t) for t in range(D_TILES) for g in pair_groups]
+        order.extend(straight[:OFFSET])
+        straight = straight[OFFSET:]
+        while straight or paired:
+            if paired:
+                order.append(paired[0])
+                paired = paired[1:]
+            if straight:
+                order.append(straight[0])
+                straight = straight[1:]
+        last_of = {}
+        for s in range(len(order)):
+            if order[s][0] in ("direct", "pair"):
+                last_of[order[s][2]] = s
 
         with tc.manual_schedule():
-            for j in range(FRONT):
-                prepare(j)
-            folded = 0
-            for first in range(FRONT, PAIRS, FRONT):
-                for l in range(folded, folded + PAIR):
-                    fold_on_vector(l)
-                folded += PAIR
-                for j in range(first, first + FRONT):
-                    prepare(j)
-            parked = []
-            for gp_l in range(L - GP_POSITIONS, L):
-                for l in range(folded, folded + PAIR):
-                    fold_on_vector(l)
-                folded += PAIR
-                parked.append(park(gp_l))
-            for fresh in parked[1:]:
-                fold_on_gpsimd(parked[0], fresh)
-            for l in range(folded, L - GP_POSITIONS):
-                fold_on_vector(l)
-            for h in range(HALVES):
-                nc.vector.tensor_max(out=best[h][:], in0=parked[0][h][:], in1=best[h][:])
-
-            shifted = []
-            grown = []
-            for h in range(HALVES):
-                v = tail.tile([P, HALF], F32, name="v")
-                nc.vector.tensor_add(out=v[:], in0=best[h][:], in1=bias[:, HALF * h : HALF * (h + 1)])
-                low = tail.tile([P, HALF], F32, name="low")
-                nc.vector.tensor_scalar_min(out=low[:], in0=v[:], scalar1=0.0)
-                e = tail.tile([P, HALF], F32, name="e")
-                nc.scalar.activation(out=e[:], in_=low[:], func=EXP)
-                shifted.append(v)
-                grown.append(e)
-            for h in range(HALVES):
-                result = tail.tile([P, HALF], F32, name="result")
-                nc.vector.scalar_tensor_tensor(
-                    out=result[:],
-                    in0=grown[h][:],
-                    scalar=-1.0,
-                    in1=shifted[h][:],
-                    op0=mybir.AluOpType.add,
-                    op1=mybir.AluOpType.max,
-                )
-                nc.sync.dma_start(out=out[:, HALF * h : HALF * (h + 1)], in_=result[:])
+            produced = set()
+            written = set()
+            span = max(LEAD.values())
+            bias_ready = False
+            n_steps = len(order)
+            bias_step = {t: last_of[t] + BIAS_LAG for t in range(D_TILES)}
+            back_step = {t: min(last_of[t] + BACK_LAG, max(last_of[t] + BIAS_LAG, n_steps - 3)) for t in range(D_TILES)}
+            store_step = {g: min(back_step[g[1] - 1] + LAST_LAG, n_steps) for g in FINISH_GROUPS}
+            for s in range(n_steps + 1):
+                for j in range(s, min(len(order), s + span + 1)):
+                    item = order[j]
+                    if item in produced or j - LEAD[item[0]] > s:
+                        continue
+                    if all(need in written for need in needs(item)):
+                        produce(item)
+                        produced.add(item)
+                if s < len(order):
+                    assert order[s] in produced
+                    consume(order[s])
+                    written.add(order[s])
+                if not bias_ready and s < len(order) and order[s] == ("quant", len(blocks) - 1):
+                    bias_t_ps = psum_t.tile([P, P], BF16, name="turned")
+                    nc.tensor.transpose(bias_t_ps[:], bias_rows[:], ident_bf[:])
+                    nc.scalar.copy(out=bias_cols[:], in_=bias_t_ps[:, 0:D_TILES])
+                    bias_ready = True
+                for t in range(D_TILES):
+                    if s == min(bias_step[t], n_steps):
+                        add_bias(t)
+                    if s == min(back_step[t], n_steps):
+                        turn_back(t)
+                for g in FINISH_GROUPS:
+                    if s == store_step[g]:
+                        store(g[0], g[1])

@@ -26,8 +26,8 @@ SLOTS = 4
 WORDS = F // 2
 
 PLAN = "DPPDDD"
-OFFSET = 9
-LEAD = {"quant": 4, "negate": 4, "direct": 2, "pair": 9}
+OFFSET = 4
+LEAD = {"quant": 4, "negate": 4, "direct": 2, "pair": 8}
 FINISH_GROUPS = ((0, 4), (4, 7), (7, 8))
 BIAS_LAG = 1
 BACK_LAG = 8
@@ -250,18 +250,19 @@ def tile_conceptembedmodel_pa_kernel(tc, x, conv_w_words, conv_w_scales, conv_b,
                     order.append(("direct", direct_groups[0], filled))
                     filled += 1
                 order.append(step)
-            if j == 0:
+            if not blocks[j]["negated"] and filled < D_TILES:
                 order.append(("direct", direct_groups[0], filled))
                 filled += 1
         straight = [("direct", g, t) for t in range(D_TILES) for g in direct_groups if ("direct", g, t) not in order]
         paired = [("pair", g, t) for t in range(D_TILES) for g in pair_groups]
         order.extend(straight[:OFFSET])
         straight = straight[OFFSET:]
+        n_straight, n_paired = len(straight), len(paired)
         while straight or paired:
-            if paired:
+            if paired and (not straight or len(paired) * n_straight >= len(straight) * n_paired):
                 order.append(paired[0])
                 paired = paired[1:]
-            if straight:
+            else:
                 order.append(straight[0])
                 straight = straight[1:]
         last_of = {}

@@ -90,6 +90,7 @@ def tile_conceptembedmodel_pa_kernel(tc, x, conv_w_words, conv_w_scales, conv_b,
         for block in blocks:
             block["x"] = []
         load_tile(blocks[0], 0)
+        load_tile(blocks[0], 1)
         scale_rows = conv_w_scales.rearrange("g q n -> (g q) n")
         for quadrant in range(4):
             nc.sync.dma_start(
@@ -101,7 +102,6 @@ def tile_conceptembedmodel_pa_kernel(tc, x, conv_w_words, conv_w_scales, conv_b,
             out=w_words[:].bitcast(I32),
             in_=conv_w_words.rearrange("g p n -> (g p) n").bitcast(I32),
         )
-        load_tile(blocks[0], 1)
         for block in blocks[1:]:
             load_tile(block, 0)
             load_tile(block, 1)

@@ -41,6 +41,7 @@ def tile_conceptembedmodel_pa_kernel(tc, x, conv_w_words, conv_w_scales, conv_b,
     with ExitStack() as ctx:
         const = ctx.enter_context(tc.tile_pool(name="const", bufs=1))
         x_pool = ctx.enter_context(tc.tile_pool(name="x_pool", bufs=16))
+        x_big = ctx.enter_context(tc.tile_pool(name="x_big", bufs=8))
         stage = ctx.enter_context(tc.tile_pool(name="stage", bufs=8))
         keep = ctx.enter_context(tc.tile_pool(name="keep", bufs=12))
         sums = ctx.enter_context(tc.tile_pool(name="sums", bufs=8))
@@ -102,9 +103,14 @@ def tile_conceptembedmodel_pa_kernel(tc, x, conv_w_words, conv_w_scales, conv_b,
             out=w_words[:].bitcast(I32),
             in_=conv_w_words.rearrange("g p n -> (g p) n").bitcast(I32),
         )
-        for block in blocks[1:]:
-            load_tile(block, 0)
-            load_tile(block, 1)
+        for j in range(1, len(blocks)):
+            if j < 2:
+                load_tile(blocks[j], 0)
+                load_tile(blocks[j], 1)
+            else:
+                x_block = x_big.tile([P, 4 * F], BF16, name="x_block")
+                nc.sync.dma_start(out=x_block[:], in_=blocks[j]["view"])
+                blocks[j]["x"] = [x_block[:, 0 : 2 * F], x_block[:, 2 * F : 4 * F]]
         nc.sync.dma_start(out=bias_rows[0:D_TILES, :], in_=conv_b.rearrange("(t p) -> t p", p=P))
 
         best = [const.tile([P, B], F32, name="best%d" % t) for t in range(D_TILES)]
@@ -115,7 +121,7 @@ def tile_conceptembedmodel_pa_kernel(tc, x, conv_w_words, conv_w_scales, conv_b,
             grouped = stage.tile([P, SLOTS * P * 4], BF16, align_bytes=64, name="grouped")
             block["grouped"] = grouped
             for k in range(2):
-                x_words = block["x"][k][:].bitcast(F32)
+                x_words = block["x"][k][:, :].bitcast(F32)
                 if (2 * j + k) % 5 in (0, 2):
                     turned = psum_t.tile([P, 2, 2, P], F32, name="turned")
                 else:

@@ -26,7 +26,7 @@ SLOTS = 4
 WORDS = F // 2
 
 PLAN = "DPPDDD"
-OFFSET = 4
+OFFSET = 3
 LEAD = {"quant": 4, "negate": 4, "direct": 2, "pair": 8}
 FINISH_GROUPS = ((0, 4), (4, 7), (7, 8))
 BIAS_LAG = 1

@@ -14,24 +14,31 @@ EXP = mybir.ActivationFunctionType.Exp
 RELU = mybir.ActivationFunctionType.Relu
 IDENTITY = mybir.ActivationFunctionType.Identity
 MULT = mybir.AluOpType.mult
-ADD = mybir.AluOpType.add
 MAX = mybir.AluOpType.max
-MIN = mybir.AluOpType.min
 
 P = 128
 B, L, F, D = 128, 32, 512, 1024
+PACK = 4
+WORDS = F // 2
 D_TILES = D // P
 COLS = 512
-SLOTS = 4
-WORDS = F // 2
+ROWS_EACH = COLS // P
+TILES = 2
 
-PLAN = "DPPDDD"
-OFFSET = 3
-LEAD = {"quant": 4, "negate": 4, "direct": 2, "pair": 8}
+PLAN = "SPPSSS"
+SEQUENCES = {"S": COLS // L, "P": 2 * COLS // L}
+BLOCKS = {"S": 1, "P": 2}
+N_BLOCKS = sum([BLOCKS[kind] for kind in PLAN])
+N_PAIR_GROUPS = len([kind for kind in PLAN if kind == "P"])
+TILE_LOADS = 2
+
+LEAD = {"quantise": 4, "negate": 4, "straight": 2, "pair": 8}
+STRAIGHT_FIRST = 3
+
 FINISH_GROUPS = ((0, 4), (4, 7), (7, 8))
 BIAS_LAG = 1
 BACK_LAG = 8
-LAST_LAG = 6
+STORE_LAG = 6
 
 FLOPS = 2 * B * L * F * D
 
@@ -40,13 +47,14 @@ def tile_conceptembedmodel_pa_kernel(tc, x, conv_w_words, conv_w_scales, conv_b,
     nc = tc.nc
     with ExitStack() as ctx:
         const = ctx.enter_context(tc.tile_pool(name="const", bufs=1))
-        x_pool = ctx.enter_context(tc.tile_pool(name="x_pool", bufs=16))
-        x_big = ctx.enter_context(tc.tile_pool(name="x_big", bufs=8))
-        stage = ctx.enter_context(tc.tile_pool(name="stage", bufs=8))
-        keep = ctx.enter_context(tc.tile_pool(name="keep", bufs=12))
-        sums = ctx.enter_context(tc.tile_pool(name="sums", bufs=8))
+        x_pool = ctx.enter_context(tc.tile_pool(name="x_pool", bufs=TILES * TILE_LOADS))
+        x_big = ctx.enter_context(tc.tile_pool(name="x_big", bufs=N_BLOCKS - TILE_LOADS))
+        stage = ctx.enter_context(tc.tile_pool(name="stage", bufs=N_BLOCKS))
+        minus_pool = ctx.enter_context(tc.tile_pool(name="minus_pool", bufs=N_PAIR_GROUPS))
+        keep = ctx.enter_context(tc.tile_pool(name="keep", bufs=N_BLOCKS))
+        sums = ctx.enter_context(tc.tile_pool(name="sums", bufs=LEAD["pair"]))
         rises = ctx.enter_context(tc.tile_pool(name="rises", bufs=6))
-        fin = ctx.enter_context(tc.tile_pool(name="fin", bufs=3))
+        fin = ctx.enter_context(tc.tile_pool(name="fin", bufs=len(FINISH_GROUPS)))
         psum_t = ctx.enter_context(tc.psum_pool(name="psum_t", bufs=2))
         psum_v = ctx.enter_context(tc.psum_pool(name="psum_v", bufs=3))
         psum_s = ctx.enter_context(tc.psum_pool(name="psum_s", bufs=3))
@@ -69,29 +77,30 @@ def tile_conceptembedmodel_pa_kernel(tc, x, conv_w_words, conv_w_scales, conv_b,
         blocks = []
         b0 = 0
         for kind in PLAN:
-            width = 16 if kind == "D" else 32
-            n_blocks = 1 if kind == "D" else 2
-            view = rows[L * b0 : L * (b0 + width), :].rearrange("(p n) f -> p (n f)", n=SLOTS * n_blocks)
-            group = {"kind": kind, "b0": b0, "width": width, "blocks": []}
-            for a in range(n_blocks):
+            view = rows[L * b0 : L * (b0 + SEQUENCES[kind]), :].rearrange("(p n) f -> p (n f)", n=ROWS_EACH * BLOCKS[kind])
+            group = {"kind": kind, "b0": b0, "width": SEQUENCES[kind], "blocks": []}
+            for a in range(BLOCKS[kind]):
                 group["blocks"].append(len(blocks))
                 blocks.append({
-                    "view": view[:, SLOTS * F * a : SLOTS * F * (a + 1)],
+                    "view": view[:, ROWS_EACH * F * a : ROWS_EACH * F * (a + 1)],
                     "negated": kind == "P" and a == 0,
                 })
             groups.append(group)
-            b0 += width
+            b0 += SEQUENCES[kind]
         assert b0 == B
+        straight_groups = [g for g in range(len(groups)) if groups[g]["kind"] == "S"]
+        pair_groups = [g for g in range(len(groups)) if groups[g]["kind"] == "P"]
 
-        def load_tile(block, k):
-            x_tile = x_pool.tile([P, 2 * F], BF16, name="x_tile")
-            nc.sync.dma_start(out=x_tile[:], in_=block["view"][:, 2 * F * k : 2 * F * (k + 1)])
-            block["x"].append(x_tile)
+        tile_width = ROWS_EACH * F // TILES
 
-        for block in blocks:
+        def load_by_tiles(block):
             block["x"] = []
-        load_tile(blocks[0], 0)
-        load_tile(blocks[0], 1)
+            for k in range(TILES):
+                x_tile = x_pool.tile([P, tile_width], BF16, name="x_tile")
+                nc.sync.dma_start(out=x_tile[:], in_=block["view"][:, tile_width * k : tile_width * (k + 1)])
+                block["x"].append(x_tile[:, :])
+
+        load_by_tiles(blocks[0])
         scale_rows = conv_w_scales.rearrange("g q n -> (g q) n")
         for quadrant in range(4):
             nc.sync.dma_start(
@@ -103,26 +112,25 @@ def tile_conceptembedmodel_pa_kernel(tc, x, conv_w_words, conv_w_scales, conv_b,
             out=w_words[:].bitcast(I32),
             in_=conv_w_words.rearrange("g p n -> (g p) n").bitcast(I32),
         )
-        for j in range(1, len(blocks)):
-            if j < 2:
-                load_tile(blocks[j], 0)
-                load_tile(blocks[j], 1)
+        for j in range(1, N_BLOCKS):
+            if j < TILE_LOADS:
+                load_by_tiles(blocks[j])
             else:
-                x_block = x_big.tile([P, 4 * F], BF16, name="x_block")
+                x_block = x_big.tile([P, TILES * tile_width], BF16, name="x_block")
                 nc.sync.dma_start(out=x_block[:], in_=blocks[j]["view"])
-                blocks[j]["x"] = [x_block[:, 0 : 2 * F], x_block[:, 2 * F : 4 * F]]
+                blocks[j]["x"] = [x_block[:, tile_width * k : tile_width * (k + 1)] for k in range(TILES)]
         nc.sync.dma_start(out=bias_rows[0:D_TILES, :], in_=conv_b.rearrange("(t p) -> t p", p=P))
 
         best = [const.tile([P, B], F32, name="best%d" % t) for t in range(D_TILES)]
         bias_cols = const.tile([P, D_TILES], F32)
 
-        def turn(j):
+        def transpose_block(j):
             block = blocks[j]
-            grouped = stage.tile([P, SLOTS * P * 4], BF16, align_bytes=64, name="grouped")
+            grouped = stage.tile([P, COLS * PACK], BF16, align_bytes=64, name="grouped")
             block["grouped"] = grouped
-            for k in range(2):
-                x_words = block["x"][k][:, :].bitcast(F32)
-                if (2 * j + k) % 5 in (0, 2):
+            for k in range(TILES):
+                x_words = block["x"][k].bitcast(F32)
+                if (TILES * j + k) % 5 in (0, 2):
                     turned = psum_t.tile([P, 2, 2, P], F32, name="turned")
                 else:
                     turned = psum_s.tile([P, 2, 2, P], F32, name="zs")
@@ -134,26 +142,27 @@ def tile_conceptembedmodel_pa_kernel(tc, x, conv_w_words, conv_w_scales, conv_b,
                             ident[:],
                         )
                 nc.scalar.copy(
-                    out=grouped[:, 2 * F * k : 2 * F * (k + 1)].bitcast(F32).rearrange("p (i c u) -> p i c u", i=2, u=2),
+                    out=grouped[:, tile_width * k : tile_width * (k + 1)].bitcast(F32).rearrange("p (i c u) -> p i c u", i=2, u=2),
                     in_=turned[:].rearrange("p i u c -> p i c u"),
                 )
 
-        def quantise(source):
-            codes = keep.tile([P, COLS], U32, align_bytes=64, name="codes")
-            scales = keep.tile([P, COLS], U8, align_bytes=64, name="scales")
-            nc.vector.quantize_mx(out=codes[:].bitcast(FP8X4), scales=scales[:], in_=source[:])
-            return (codes, scales)
-
-        def negate(j):
+        def negate_block(j):
             block = blocks[j]
-            minus = stage.tile([P, SLOTS * P * 4], BF16, align_bytes=64, name="minus")
+            minus = minus_pool.tile([P, COLS * PACK], BF16, align_bytes=64, name="minus")
             nc.vector.tensor_scalar_mul(out=minus[:], in0=block["grouped"][:], scalar1=-1.0)
             block["grouped"] = minus
 
-        def multiply(z, t, operand, start, stop):
-            codes, scales = operand
+        def quantise_block(j):
+            block = blocks[j]
+            codes = keep.tile([P, COLS], U32, align_bytes=64, name="codes")
+            scales = keep.tile([P, COLS], U8, align_bytes=64, name="scales")
+            nc.vector.quantize_mx(out=codes[:].bitcast(FP8X4), scales=scales[:], in_=block["grouped"][:])
+            block["codes"] = (codes, scales)
+
+        def multiply(bank, t, j, start, stop):
+            codes, scales = blocks[j]["codes"]
             nc.tensor.matmul_mx(
-                out=z[:],
+                out=bank[:],
                 lhsT=w_words[:, 2 * P * t : 2 * P * (t + 1)].bitcast(FP4X4),
                 lhsT_scale=w_scales[:, P * t : P * (t + 1)],
                 rhs=codes[:].bitcast(FP8X4),
@@ -162,56 +171,48 @@ def tile_conceptembedmodel_pa_kernel(tc, x, conv_w_words, conv_w_scales, conv_b,
                 stop=stop,
             )
 
-        def fold(source, group, t):
-            nc.vector.tensor_reduce(
-                out=best[t][:, group["b0"] : group["b0"] + group["width"]],
-                in_=source[:].rearrange("p (i c q) -> p c i q", i=SLOTS, c=group["width"]),
-                axis=mybir.AxisListType.XY,
-                op=MAX,
-            )
+        ready = {}
 
-        made = {}
-
-        def produce(item):
-            kind = item[0]
-            if kind == "negate" or (kind == "quant" and not blocks[item[1]]["negated"]):
-                turn(item[1])
-            elif kind == "direct":
-                group, t = groups[item[1]], item[2]
+        def write_producers(step):
+            kind = step[0]
+            if kind == "negate" or (kind == "quantise" and not blocks[step[1]]["negated"]):
+                transpose_block(step[1])
+            elif kind == "straight":
                 z = psum_v.tile([P, COLS], F32, name="z")
-                multiply(z, t, blocks[group["blocks"][0]]["codes"], True, True)
-                made[item] = z
+                multiply(z, step[2], groups[step[1]]["blocks"][0], True, True)
+                ready[step] = z
             elif kind == "pair":
-                group, t = groups[item[1]], item[2]
-                first, second = blocks[group["blocks"][0]], blocks[group["blocks"][1]]
+                first, second = groups[step[1]]["blocks"]
                 z_first = psum_s.tile([P, COLS], F32, name="zs")
-                multiply(z_first, t, first["codes"], True, True)
+                multiply(z_first, step[2], first, True, True)
                 z_rise = psum_s.tile([P, COLS], F32, name="zs")
-                multiply(z_rise, t, second["codes"], True, False)
-                multiply(z_rise, t, first["codes"], False, True)
+                multiply(z_rise, step[2], second, True, False)
+                multiply(z_rise, step[2], first, False, True)
                 total = sums.tile([P, COLS], F32, name="total")
                 nc.scalar.copy(out=total[:], in_=z_first[:])
                 rise = rises.tile([P, COLS], F32, name="rise")
                 nc.scalar.activation(out=rise[:], in_=z_rise[:], func=RELU)
                 nc.gpsimd.tensor_sub(out=total[:], in0=rise[:], in1=total[:])
-                made[item] = total
+                ready[step] = total
 
-        def consume(item):
-            kind = item[0]
-            if kind == "quant":
-                blocks[item[1]]["codes"] = quantise(blocks[item[1]]["grouped"])
+        def write_step(step):
+            kind = step[0]
+            if kind == "quantise":
+                quantise_block(step[1])
             elif kind == "negate":
-                negate(item[1])
+                negate_block(step[1])
             else:
-                fold(made[item], groups[item[1]], item[2])
+                group = groups[step[1]]
+                nc.vector.tensor_reduce(
+                    out=best[step[2]][:, group["b0"] : group["b0"] + group["width"]],
+                    in_=ready[step][:].rearrange("p (i c q) -> p c i q", i=ROWS_EACH, c=group["width"]),
+                    axis=mybir.AxisListType.XY,
+                    op=MAX,
+                )
 
-        def needs(item):
-            kind = item[0]
-            if kind == "direct":
-                return [("quant", groups[item[1]]["blocks"][0])]
-            if kind == "pair":
-                first, second = groups[item[1]]["blocks"]
-                return [("quant", first), ("quant", second)]
+        def codes_needed(step):
+            if step[0] in ("straight", "pair"):
+                return [("quantise", j) for j in groups[step[1]]["blocks"]]
             return []
 
         shifted = {}
@@ -245,24 +246,19 @@ def tile_conceptembedmodel_pa_kernel(tc, x, conv_w_words, conv_w_scales, conv_b,
             )
             nc.sync.dma_start(out=out[:, P * t0 : P * t1], in_=final[:, 0:width])
 
-        direct_groups = [g for g in range(len(groups)) if groups[g]["kind"] == "D"]
-        pair_groups = [g for g in range(len(groups)) if groups[g]["kind"] == "P"]
         order = []
-        filled = 0
-        for j in range(len(blocks)):
-            steps = [("negate", j), ("quant", j)] if blocks[j]["negated"] else [("quant", j)]
-            for step in steps:
-                if step != steps[0] and filled < D_TILES:
-                    order.append(("direct", direct_groups[0], filled))
-                    filled += 1
-                order.append(step)
-            if not blocks[j]["negated"] and filled < D_TILES:
-                order.append(("direct", direct_groups[0], filled))
-                filled += 1
-        straight = [("direct", g, t) for t in range(D_TILES) for g in direct_groups if ("direct", g, t) not in order]
+        first_group = [("straight", straight_groups[0], t) for t in range(D_TILES)]
+        for j in range(N_BLOCKS):
+            if blocks[j]["negated"]:
+                order.extend([("negate", j), first_group[0], ("quantise", j)])
+            else:
+                order.extend([("quantise", j), first_group[0]])
+            first_group = first_group[1:]
+        assert not first_group
+        straight = [("straight", g, t) for t in range(D_TILES) for g in straight_groups[1:]]
         paired = [("pair", g, t) for t in range(D_TILES) for g in pair_groups]
-        order.extend(straight[:OFFSET])
-        straight = straight[OFFSET:]
+        order.extend(straight[:STRAIGHT_FIRST])
+        straight = straight[STRAIGHT_FIRST:]
         n_straight, n_paired = len(straight), len(paired)
         while straight or paired:
             if paired and (not straight or len(paired) * n_straight >= len(straight) * n_paired):
@@ -271,41 +267,38 @@ def tile_conceptembedmodel_pa_kernel(tc, x, conv_w_words, conv_w_scales, conv_b,
             else:
                 order.append(straight[0])
                 straight = straight[1:]
-        last_of = {}
-        for s in range(len(order)):
-            if order[s][0] in ("direct", "pair"):
-                last_of[order[s][2]] = s
+        n_steps = len(order)
+        last_reduce = {}
+        for s in range(n_steps):
+            if order[s][0] in ("straight", "pair"):
+                last_reduce[order[s][2]] = s
+
+        bias_step = {t: last_reduce[t] + BIAS_LAG for t in range(D_TILES)}
+        back_step = {
+            t: min(last_reduce[t] + BACK_LAG, max(bias_step[t], n_steps - 1 - LEAD["straight"])) for t in range(D_TILES)
+        }
+        store_step = {g: min(back_step[g[1] - 1] + STORE_LAG, n_steps) for g in FINISH_GROUPS}
 
         with tc.manual_schedule():
             produced = set()
             written = set()
-            span = max(LEAD.values())
-            bias_ready = False
-            n_steps = len(order)
-            bias_step = {t: last_of[t] + BIAS_LAG for t in range(D_TILES)}
-            back_step = {t: min(last_of[t] + BACK_LAG, max(last_of[t] + BIAS_LAG, n_steps - 3)) for t in range(D_TILES)}
-            store_step = {g: min(back_step[g[1] - 1] + LAST_LAG, n_steps) for g in FINISH_GROUPS}
             for s in range(n_steps + 1):
-                for j in range(s, min(len(order), s + span + 1)):
-                    item = order[j]
-                    if item in produced or j - LEAD[item[0]] > s:
-                        continue
-                    if all(need in written for need in needs(item)):
-                        produce(item)
-                        produced.add(item)
-                if s < len(order):
-                    assert order[s] in produced
-                    consume(order[s])
+                for ahead in range(s, min(n_steps, s + max(LEAD.values()) + 1)):
+                    step = order[ahead]
+                    if step not in produced and ahead - LEAD[step[0]] <= s and all(q in written for q in codes_needed(step)):
+                        write_producers(step)
+                        produced.add(step)
+                if s < n_steps:
+                    write_step(order[s])
                     written.add(order[s])
-                if not bias_ready and s < len(order) and order[s] == ("quant", len(blocks) - 1):
-                    bias_t_ps = psum_t.tile([P, P], BF16, name="turned")
-                    nc.tensor.transpose(bias_t_ps[:], bias_rows[:], ident_bf[:])
-                    nc.scalar.copy(out=bias_cols[:], in_=bias_t_ps[:, 0:D_TILES])
-                    bias_ready = True
+                    if order[s] == ("quantise", N_BLOCKS - 1):
+                        bias_turned = psum_t.tile([P, P], BF16, name="turned")
+                        nc.tensor.transpose(bias_turned[:], bias_rows[:], ident_bf[:])
+                        nc.scalar.copy(out=bias_cols[:], in_=bias_turned[:, 0:D_TILES])
                 for t in range(D_TILES):
-                    if s == min(bias_step[t], n_steps):
+                    if s == bias_step[t]:
                         add_bias(t)
-                    if s == min(back_step[t], n_steps):
+                    if s == back_step[t]:
                         turn_back(t)
                 for g in FINISH_GROUPS:
                     if s == store_step[g]:

@@ -72,6 +72,9 @@ def tile_conceptembedmodel_pa_kernel(tc, x, conv_w_words, conv_w_scales, conv_b,
         bias_rows = const.tile([P, P], BF16)
         nc.gpsimd.memset(bias_rows[:], 0.0)
 
+        zeros = const.tile([P, COLS], BF16)
+        nc.vector.memset(zeros[:], 0.0)
+
         rows = x.rearrange("b l f -> (b l) f")
         groups = []
         blocks = []
@@ -280,6 +283,9 @@ def tile_conceptembedmodel_pa_kernel(tc, x, conv_w_words, conv_w_scales, conv_b,
         store_step = {g: min(back_step[g[1] - 1] + STORE_LAG, n_steps) for g in FINISH_GROUPS}
 
         with tc.manual_schedule():
+            idle_bank = psum_v.tile([P, COLS], F32, name="z")
+            for warm_up in range(4):
+                nc.tensor.matmul(out=idle_bank[:], lhsT=zeros[:, 0:P], rhs=zeros[:], start=True, stop=True)
             produced = set()
             written = set()
             for s in range(n_steps + 1):

@@ -13,7 +13,8 @@ FP4X4 = mybir.dt.float4_e2m1fn_x4
 EXP = mybir.ActivationFunctionType.Exp
 RELU = mybir.ActivationFunctionType.Relu
 IDENTITY = mybir.ActivationFunctionType.Identity
-MULT = mybir.AluOpType.mult
+MIN = mybir.AluOpType.min
+ADD = mybir.AluOpType.add
 MAX = mybir.AluOpType.max
 
 P = 128
@@ -32,10 +33,16 @@ N_BLOCKS = sum([BLOCKS[kind] for kind in PLAN])
 N_PAIR_GROUPS = len([kind for kind in PLAN if kind == "P"])
 TILE_LOADS = 2
 
-LEAD = {"quantise": 4, "negate": 4, "straight": 2, "pair": 8}
+HALVES = 2
+HALF = COLS // HALVES
+HALF_SEQUENCES = HALF // L
+HALF_TILES = 3
+
+LEAD = {"turn": 0, "lift": 0, "quantise": 4, "negate": 4, "half": 5, "straight": 2, "pair": 8}
 STRAIGHT_FIRST = 3
 
 FINISH_GROUPS = ((0, 4), (4, 7), (7, 8))
+BIAS_AFTER = 3
 BIAS_LAG = 1
 BACK_LAG = 8
 STORE_LAG = 6
@@ -76,21 +83,28 @@ def tile_conceptembedmodel_pa_kernel(tc, x, conv_w_words, conv_w_scales, conv_b,
         nc.vector.memset(zeros[:], 0.0)
 
         rows = x.rearrange("b l f -> (b l) f")
+        first_sequence = {"S": 0, "P": SEQUENCES["S"] * len([kind for kind in PLAN if kind == "S"])}
+        n_straight_sequences = first_sequence["P"]
         groups = []
         blocks = []
-        b0 = 0
         for kind in PLAN:
+            b0 = first_sequence[kind]
             view = rows[L * b0 : L * (b0 + SEQUENCES[kind]), :].rearrange("(p n) f -> p (n f)", n=ROWS_EACH * BLOCKS[kind])
             group = {"kind": kind, "b0": b0, "width": SEQUENCES[kind], "blocks": []}
             for a in range(BLOCKS[kind]):
                 group["blocks"].append(len(blocks))
+                tile_run = ROWS_EACH * F // TILES
+                tile_views = [view[:, ROWS_EACH * F * a + tile_run * k : ROWS_EACH * F * a + tile_run * (k + 1)] for k in range(TILES)]
+                if not blocks:
+                    tile_views = [rows[HALF * h : HALF * (h + 1), :].rearrange("(p n) f -> p (n f)", n=ROWS_EACH // HALVES) for h in range(HALVES)]
                 blocks.append({
                     "view": view[:, ROWS_EACH * F * a : ROWS_EACH * F * (a + 1)],
+                    "tile_views": tile_views,
                     "negated": kind == "P" and a == 0,
                 })
             groups.append(group)
-            b0 += SEQUENCES[kind]
-        assert b0 == B
+            first_sequence[kind] += SEQUENCES[kind]
+        assert first_sequence["P"] == B
         straight_groups = [g for g in range(len(groups)) if groups[g]["kind"] == "S"]
         pair_groups = [g for g in range(len(groups)) if groups[g]["kind"] == "P"]
 
@@ -100,7 +114,7 @@ def tile_conceptembedmodel_pa_kernel(tc, x, conv_w_words, conv_w_scales, conv_b,
             block["x"] = []
             for k in range(TILES):
                 x_tile = x_pool.tile([P, tile_width], BF16, name="x_tile")
-                nc.sync.dma_start(out=x_tile[:], in_=block["view"][:, tile_width * k : tile_width * (k + 1)])
+                nc.sync.dma_start(out=x_tile[:], in_=block["tile_views"][k])
                 block["x"].append(x_tile[:, :])
 
         load_by_tiles(blocks[0])
@@ -116,38 +130,64 @@ def tile_conceptembedmodel_pa_kernel(tc, x, conv_w_words, conv_w_scales, conv_b,
             in_=conv_w_words.rearrange("g p n -> (g p) n").bitcast(I32),
         )
         for j in range(1, N_BLOCKS):
+            if j == N_BLOCKS // 2:
+                nc.sync.dma_start(out=bias_rows[0:D_TILES, :], in_=conv_b.rearrange("(t p) -> t p", p=P))
             if j < TILE_LOADS:
                 load_by_tiles(blocks[j])
             else:
                 x_block = x_big.tile([P, TILES * tile_width], BF16, name="x_block")
                 nc.sync.dma_start(out=x_block[:], in_=blocks[j]["view"])
                 blocks[j]["x"] = [x_block[:, tile_width * k : tile_width * (k + 1)] for k in range(TILES)]
-        nc.sync.dma_start(out=bias_rows[0:D_TILES, :], in_=conv_b.rearrange("(t p) -> t p", p=P))
 
         best = [const.tile([P, B], F32, name="best%d" % t) for t in range(D_TILES)]
         bias_cols = const.tile([P, D_TILES], F32)
 
-        def transpose_block(j):
+        def copy_out(engine_copy, block, turned, k, i0, n):
+            width = PACK * P
+            first = 2 * k + i0
+            engine_copy(
+                out=block["grouped"][:, width * first : width * (first + n)].bitcast(F32).rearrange("p (i c u) -> p i c u", i=n, u=2),
+                in_=turned[:, 0:n, :, :].rearrange("p i u c -> p i c u"),
+            )
+
+        def turn_rows(j, k, i0, n):
             block = blocks[j]
-            grouped = stage.tile([P, COLS * PACK], BF16, align_bytes=64, name="grouped")
-            block["grouped"] = grouped
+            if "grouped" not in block:
+                grouped = stage.tile([P, COLS * PACK], BF16, align_bytes=64, name="grouped")
+                block["grouped"] = grouped
+            x_words = block["x"][k].bitcast(F32)
+            if len(turns) % 5 in (0, 2):
+                turned = psum_t.tile([P, 2, 2, P], F32, name="turned")
+            else:
+                turned = psum_s.tile([P, 2, 2, P], F32, name="zs")
+            turns.append(turned)
+            for i in range(n):
+                for u in range(2):
+                    nc.tensor.transpose(
+                        turned[:, i, u, :],
+                        x_words[:, WORDS * (i0 + i) + u : WORDS * (i0 + i + 1) : 2],
+                        ident[:],
+                    )
+            return turned
+
+        turns = []
+        lifts = []
+
+        def turn(j, k):
+            block = blocks[j]
+            if k in block.get("done", []):
+                return
+            block.setdefault("done", []).append(k)
+            if (j, k) == (0, 0):
+                copy_out(nc.scalar.copy, block, turn_rows(0, 0, 0, 1), 0, 0, 1)
+                lifts.append(turn_rows(0, 0, 1, 1))
+            else:
+                copy_out(nc.scalar.copy, block, turn_rows(j, k, 0, 2), k, 0, 2)
+
+        def transpose_block(j):
             for k in range(TILES):
-                x_words = block["x"][k].bitcast(F32)
-                if (TILES * j + k) % 5 in (0, 2):
-                    turned = psum_t.tile([P, 2, 2, P], F32, name="turned")
-                else:
-                    turned = psum_s.tile([P, 2, 2, P], F32, name="zs")
-                for i in range(2):
-                    for u in range(2):
-                        nc.tensor.transpose(
-                            turned[:, i, u, :],
-                            x_words[:, WORDS * i + u : WORDS * (i + 1) : 2],
-                            ident[:],
-                        )
-                nc.scalar.copy(
-                    out=grouped[:, tile_width * k : tile_width * (k + 1)].bitcast(F32).rearrange("p (i c u) -> p i c u", i=2, u=2),
-                    in_=turned[:].rearrange("p i u c -> p i c u"),
-                )
+                if k not in blocks[j].get("done", []):
+                    turn(j, k)
 
         def negate_block(j):
             block = blocks[j]
@@ -155,21 +195,25 @@ def tile_conceptembedmodel_pa_kernel(tc, x, conv_w_words, conv_w_scales, conv_b,
             nc.vector.tensor_scalar_mul(out=minus[:], in0=block["grouped"][:], scalar1=-1.0)
             block["grouped"] = minus
 
-        def quantise_block(j):
+        def quantise_cols(j, c0, c1):
             block = blocks[j]
-            codes = keep.tile([P, COLS], U32, align_bytes=64, name="codes")
-            scales = keep.tile([P, COLS], U8, align_bytes=64, name="scales")
-            nc.vector.quantize_mx(out=codes[:].bitcast(FP8X4), scales=scales[:], in_=block["grouped"][:])
-            block["codes"] = (codes, scales)
+            if "codes" not in block:
+                codes = keep.tile([P, COLS], U32, align_bytes=64, name="codes")
+                scales = keep.tile([P, COLS], U8, align_bytes=64, name="scales")
+                block["codes"] = (codes, scales)
+            codes, scales = block["codes"]
+            nc.vector.quantize_mx(
+                out=codes[:, c0:c1].bitcast(FP8X4), scales=scales[:, c0:c1], in_=block["grouped"][:, PACK * c0 : PACK * c1]
+            )
 
-        def multiply(bank, t, j, start, stop):
+        def multiply(bank, t, j, start, stop, c0=0, c1=COLS):
             codes, scales = blocks[j]["codes"]
             nc.tensor.matmul_mx(
-                out=bank[:],
+                out=bank[:, 0 : c1 - c0],
                 lhsT=w_words[:, 2 * P * t : 2 * P * (t + 1)].bitcast(FP4X4),
                 lhsT_scale=w_scales[:, P * t : P * (t + 1)],
-                rhs=codes[:].bitcast(FP8X4),
-                rhs_scale=scales[:],
+                rhs=codes[:, c0:c1].bitcast(FP8X4),
+                rhs_scale=scales[:, c0:c1],
                 start=start,
                 stop=stop,
             )
@@ -178,8 +222,14 @@ def tile_conceptembedmodel_pa_kernel(tc, x, conv_w_words, conv_w_scales, conv_b,
 
         def write_producers(step):
             kind = step[0]
-            if kind == "negate" or (kind == "quantise" and not blocks[step[1]]["negated"]):
+            if kind == "turn":
+                turn(step[1], step[2])
+            elif kind == "negate" or (kind == "quantise" and step[1] > 0 and not blocks[step[1]]["negated"]):
                 transpose_block(step[1])
+            elif kind == "half":
+                z = psum_v.tile([P, COLS], F32, name="z")
+                multiply(z, step[2], 0, True, True, HALF * step[1], HALF * (step[1] + 1))
+                ready[step] = z
             elif kind == "straight":
                 z = psum_v.tile([P, COLS], F32, name="z")
                 multiply(z, step[2], groups[step[1]]["blocks"][0], True, True)
@@ -192,16 +242,37 @@ def tile_conceptembedmodel_pa_kernel(tc, x, conv_w_words, conv_w_scales, conv_b,
                 multiply(z_rise, step[2], second, True, False)
                 multiply(z_rise, step[2], first, False, True)
                 total = sums.tile([P, COLS], F32, name="total")
-                nc.scalar.copy(out=total[:], in_=z_first[:])
+                nc.scalar.activation(out=total[:], in_=z_first[:], func=IDENTITY, scale=-1.0, bias=bias_cols[:, step[2] : step[2] + 1])
                 rise = rises.tile([P, COLS], F32, name="rise")
                 nc.scalar.activation(out=rise[:], in_=z_rise[:], func=RELU)
-                nc.gpsimd.tensor_sub(out=total[:], in0=rise[:], in1=total[:])
+                nc.gpsimd.tensor_add(out=total[:], in0=rise[:], in1=total[:])
                 ready[step] = total
 
         def write_step(step):
             kind = step[0]
-            if kind == "quantise":
-                quantise_block(step[1])
+            if kind == "turn":
+                pass
+            elif kind == "lift":
+                copy_out(nc.vector.tensor_copy, blocks[0], lifts[0], 0, 1, 1)
+            elif kind == "quantise" and step[1] == 0:
+                quantise_cols(0, HALF * step[2], HALF * (step[2] + 1))
+            elif kind == "quantise":
+                quantise_cols(step[1], 0, COLS)
+            elif kind == "half":
+                h = step[1]
+                nc.vector.tensor_reduce(
+                    out=best[step[2]][:, HALF_SEQUENCES * h : HALF_SEQUENCES * (h + 1)],
+                    in_=ready[step][:, 0:HALF].rearrange("p (i c q) -> p c i q", i=2, c=HALF_SEQUENCES),
+                    axis=mybir.AxisListType.XY,
+                    op=MAX,
+                )
+            elif kind == "straight" and step[1] == 0:
+                nc.vector.tensor_reduce(
+                    out=best[step[2]][:, 0 : SEQUENCES["S"]].rearrange("p (h c) -> p h c", h=HALVES),
+                    in_=ready[step][:].rearrange("p (h i c q) -> p h c i q", h=HALVES, i=2, c=HALF_SEQUENCES),
+                    axis=mybir.AxisListType.XY,
+                    op=MAX,
+                )
             elif kind == "negate":
                 negate_block(step[1])
             else:
@@ -213,9 +284,14 @@ def tile_conceptembedmodel_pa_kernel(tc, x, conv_w_words, conv_w_scales, conv_b,
                     op=MAX,
                 )
 
+        def quantises(j):
+            return [("quantise", 0, h) for h in range(HALVES)] if j == 0 else [("quantise", j)]
+
         def codes_needed(step):
             if step[0] in ("straight", "pair"):
-                return [("quantise", j) for j in groups[step[1]]["blocks"]]
+                return [q for j in groups[step[1]]["blocks"] for q in quantises(j)]
+            if step[0] == "half":
+                return [("quantise", 0, step[1])]
             return []
 
         shifted = {}
@@ -223,9 +299,12 @@ def tile_conceptembedmodel_pa_kernel(tc, x, conv_w_words, conv_w_scales, conv_b,
         below = {}
 
         def add_bias(t):
-            v = fin.tile([P, B], F32, name="v")
-            nc.scalar.activation(out=v[:], in_=best[t][:], func=IDENTITY, bias=bias_cols[:, t : t + 1])
-            shifted[t] = v
+            cols = best[t][:, 0:n_straight_sequences]
+            if t == D_TILES - 1:
+                nc.vector.tensor_scalar_add(out=cols, in0=cols, scalar1=bias_cols[:, t : t + 1])
+            else:
+                nc.scalar.activation(out=cols, in_=cols, func=IDENTITY, bias=bias_cols[:, t : t + 1])
+            shifted[t] = best[t]
 
         def turn_back(t):
             t0, t1 = [g for g in FINISH_GROUPS if g[0] <= t < g[1]][0]
@@ -238,25 +317,28 @@ def tile_conceptembedmodel_pa_kernel(tc, x, conv_w_words, conv_w_scales, conv_b,
                 width = P * (t1 - t0)
                 grown = fin.tile([P, COLS], F32, name="grown")
                 nc.scalar.activation(out=grown[:, 0:width], in_=back[:, 0:width], func=EXP)
-                nc.scalar.activation(out=grown[:, 0:width], in_=grown[:, 0:width], func=RELU, bias=1.0, scale=-1.0)
+                if t1 < D_TILES:
+                    nc.gpsimd.tensor_scalar(out=grown[:, 0:width], in0=grown[:, 0:width], scalar1=1.0, scalar2=-1.0, op0=MIN, op1=ADD)
                 below[t0] = grown
 
         def store(t0, t1):
             width = P * (t1 - t0)
             final = fin.tile([P, COLS], F32, name="final")
-            nc.vector.scalar_tensor_tensor(
-                out=final[:, 0:width], in0=below[t0][:, 0:width], scalar=-1.0, in1=turned_back[t0][:, 0:width], op0=MULT, op1=MAX
-            )
+            if t1 == D_TILES:
+                nc.vector.tensor_scalar(out=below[t0][:, 0:width], in0=below[t0][:, 0:width], scalar1=1.0, scalar2=-1.0, op0=MIN, op1=ADD)
+            nc.vector.tensor_tensor(out=final[:, 0:width], in0=below[t0][:, 0:width], in1=turned_back[t0][:, 0:width], op=MAX)
             nc.sync.dma_start(out=out[:, P * t0 : P * t1], in_=final[:, 0:width])
 
-        order = []
-        first_group = [("straight", straight_groups[0], t) for t in range(D_TILES)]
-        for j in range(N_BLOCKS):
+        order = [("turn", 0, 0), ("turn", 0, 1), ("lift",), ("quantise", 0, 0)]
+        order.extend([("half", 0, 0), ("turn", 1, 0), ("half", 0, 1), ("quantise", 0, 1), ("turn", 1, 1), ("half", 0, 2), ("half", 1, 0), ("turn", 2, 0), ("half", 1, 1), ("turn", 2, 1), ("half", 1, 2)])
+        first_group = [("straight", straight_groups[0], t) for t in range(HALF_TILES, D_TILES)]
+        for j in range(1, N_BLOCKS):
+            filler = first_group[: (len(first_group) + N_BLOCKS - 1 - j) // (N_BLOCKS - j)]
+            first_group = first_group[len(filler) :]
             if blocks[j]["negated"]:
-                order.extend([("negate", j), first_group[0], ("quantise", j)])
+                order.extend([("negate", j)] + filler + [("quantise", j)])
             else:
-                order.extend([("quantise", j), first_group[0]])
-            first_group = first_group[1:]
+                order.extend([("quantise", j)] + filler)
         assert not first_group
         straight = [("straight", g, t) for t in range(D_TILES) for g in straight_groups[1:]]
         paired = [("pair", g, t) for t in range(D_TILES) for g in pair_groups]
@@ -297,7 +379,7 @@ def tile_conceptembedmodel_pa_kernel(tc, x, conv_w_words, conv_w_scales, conv_b,
                 if s < n_steps:
                     write_step(order[s])
                     written.add(order[s])
-                    if order[s] == ("quantise", N_BLOCKS - 1):
+                    if order[s] == ("quantise", BIAS_AFTER):
                         bias_turned = psum_t.tile([P, P], BF16, name="turned")
                         nc.tensor.transpose(bias_turned[:], bias_rows[:], ident_bf[:])
                         nc.scalar.copy(out=bias_cols[:], in_=bias_turned[:, 0:D_TILES])

@@ -13,6 +13,7 @@ FP4X4 = mybir.dt.float4_e2m1fn_x4
 EXP = mybir.ActivationFunctionType.Exp
 RELU = mybir.ActivationFunctionType.Relu
 IDENTITY = mybir.ActivationFunctionType.Identity
+MULT = mybir.AluOpType.mult
 MIN = mybir.AluOpType.min
 ADD = mybir.AluOpType.add
 MAX = mybir.AluOpType.max
@@ -31,6 +32,7 @@ SEQUENCES = {"S": COLS // L, "P": 2 * COLS // L}
 BLOCKS = {"S": 1, "P": 2}
 N_BLOCKS = sum([BLOCKS[kind] for kind in PLAN])
 N_PAIR_GROUPS = len([kind for kind in PLAN if kind == "P"])
+ORDER = "T00 T01 L Q00 X0 H00 T10 H01 Q01 T11 H02 H10 T20 H11 T21 H12 N1 T30 T31 S Q1 Q2 Y0 B N3 T40 T41 T50 T51 S Q3 S Q4 Y1 T60 T61 Q5 X1 S S T70 T71 Q6 X2 S S Q7 X3 S S S P S S P S P S P S P S P S S P S P S P S P S P S S P S P S P S P S P S"
 TILE_LOADS = 2
 
 HALVES = 2
@@ -38,11 +40,13 @@ HALF = COLS // HALVES
 HALF_SEQUENCES = HALF // L
 HALF_TILES = 3
 
-LEAD = {"turn": 0, "lift": 0, "quantise": 4, "negate": 4, "half": 5, "straight": 2, "pair": 8}
+LEAD = {"turn": 0, "lift": 0, "bias": 0, "quantise": 0, "negate": 0, "half": 5, "straight": 2, "pair": 8}
 STRAIGHT_FIRST = 3
 
 FINISH_GROUPS = ((0, 4), (4, 7), (7, 8))
-BIAS_AFTER = 3
+S_NEG = ()
+T_BANKS = (0, 2)
+BIAS_AFTER = 2
 BIAS_LAG = 1
 BACK_LAG = 8
 STORE_LAG = 6
@@ -98,6 +102,7 @@ def tile_conceptembedmodel_pa_kernel(tc, x, conv_w_words, conv_w_scales, conv_b,
                 if not blocks:
                     tile_views = [rows[HALF * h : HALF * (h + 1), :].rearrange("(p n) f -> p (n f)", n=ROWS_EACH // HALVES) for h in range(HALVES)]
                 blocks.append({
+                    "index": len(blocks),
                     "view": view[:, ROWS_EACH * F * a : ROWS_EACH * F * (a + 1)],
                     "tile_views": tile_views,
                     "negated": kind == "P" and a == 0,
@@ -145,9 +150,17 @@ def tile_conceptembedmodel_pa_kernel(tc, x, conv_w_words, conv_w_scales, conv_b,
         def copy_out(engine_copy, block, turned, k, i0, n):
             width = PACK * P
             first = 2 * k + i0
+            if block["negated"] and block["index"] in S_NEG:
+                nc.scalar.activation(
+                    out=block["grouped"][:, width * first : width * (first + n)].rearrange("p (c u e) -> p c u e", u=2, e=2),
+                    in_=turned[:].rearrange("p u i c -> p u (i c)").bitcast(BF16).rearrange("p u (c e) -> p c u e", e=2),
+                    func=IDENTITY,
+                    scale=-1.0,
+                )
+                return
             engine_copy(
-                out=block["grouped"][:, width * first : width * (first + n)].bitcast(F32).rearrange("p (i c u) -> p i c u", i=n, u=2),
-                in_=turned[:, 0:n, :, :].rearrange("p i u c -> p i c u"),
+                out=block["grouped"][:, width * first : width * (first + n)].bitcast(F32).rearrange("p (c u) -> p c u", u=2),
+                in_=turned[:].rearrange("p u i c -> p (i c) u"),
             )
 
         def turn_rows(j, k, i0, n):
@@ -156,15 +169,15 @@ def tile_conceptembedmodel_pa_kernel(tc, x, conv_w_words, conv_w_scales, conv_b,
                 grouped = stage.tile([P, COLS * PACK], BF16, align_bytes=64, name="grouped")
                 block["grouped"] = grouped
             x_words = block["x"][k].bitcast(F32)
-            if len(turns) % 5 in (0, 2):
-                turned = psum_t.tile([P, 2, 2, P], F32, name="turned")
+            if len(turns) % 5 in T_BANKS:
+                turned = psum_t.tile([P, 2, n, P], F32, name="turned")
             else:
-                turned = psum_s.tile([P, 2, 2, P], F32, name="zs")
+                turned = psum_s.tile([P, 2, n, P], F32, name="zs")
             turns.append(turned)
             for i in range(n):
                 for u in range(2):
                     nc.tensor.transpose(
-                        turned[:, i, u, :],
+                        turned[:, u, i, :],
                         x_words[:, WORDS * (i0 + i) + u : WORDS * (i0 + i + 1) : 2],
                         ident[:],
                     )
@@ -224,8 +237,12 @@ def tile_conceptembedmodel_pa_kernel(tc, x, conv_w_words, conv_w_scales, conv_b,
             kind = step[0]
             if kind == "turn":
                 turn(step[1], step[2])
-            elif kind == "negate" or (kind == "quantise" and step[1] > 0 and not blocks[step[1]]["negated"]):
-                transpose_block(step[1])
+            elif kind == "bias":
+                bias_turned = psum_t.tile([P, P], BF16, name="turned")
+                nc.tensor.transpose(bias_turned[:], bias_rows[:], ident_bf[:])
+                nc.scalar.copy(out=bias_cols[:], in_=bias_turned[:, 0:D_TILES])
+            elif kind in ("negate", "quantise"):
+                assert len(blocks[step[1]]["x"]) == len(blocks[step[1]]["done"])
             elif kind == "half":
                 z = psum_v.tile([P, COLS], F32, name="z")
                 multiply(z, step[2], 0, True, True, HALF * step[1], HALF * (step[1] + 1))
@@ -250,7 +267,7 @@ def tile_conceptembedmodel_pa_kernel(tc, x, conv_w_words, conv_w_scales, conv_b,
 
         def write_step(step):
             kind = step[0]
-            if kind == "turn":
+            if kind in ("turn", "bias"):
                 pass
             elif kind == "lift":
                 copy_out(nc.vector.tensor_copy, blocks[0], lifts[0], 0, 1, 1)
@@ -318,7 +335,7 @@ def tile_conceptembedmodel_pa_kernel(tc, x, conv_w_words, conv_w_scales, conv_b,
                 grown = fin.tile([P, COLS], F32, name="grown")
                 nc.scalar.activation(out=grown[:, 0:width], in_=back[:, 0:width], func=EXP)
                 if t1 < D_TILES:
-                    nc.gpsimd.tensor_scalar(out=grown[:, 0:width], in0=grown[:, 0:width], scalar1=1.0, scalar2=-1.0, op0=MIN, op1=ADD)
+                    nc.scalar.activation(out=grown[:, 0:width], in_=grown[:, 0:width], func=RELU, bias=1.0, scale=-1.0)
                 below[t0] = grown
 
         def store(t0, t1):
@@ -326,24 +343,34 @@ def tile_conceptembedmodel_pa_kernel(tc, x, conv_w_words, conv_w_scales, conv_b,
             final = fin.tile([P, COLS], F32, name="final")
             if t1 == D_TILES:
                 nc.vector.tensor_scalar(out=below[t0][:, 0:width], in0=below[t0][:, 0:width], scalar1=1.0, scalar2=-1.0, op0=MIN, op1=ADD)
-            nc.vector.tensor_tensor(out=final[:, 0:width], in0=below[t0][:, 0:width], in1=turned_back[t0][:, 0:width], op=MAX)
+                nc.vector.tensor_tensor(out=final[:, 0:width], in0=below[t0][:, 0:width], in1=turned_back[t0][:, 0:width], op=MAX)
+            else:
+                nc.vector.scalar_tensor_tensor(
+                    out=final[:, 0:width], in0=below[t0][:, 0:width], scalar=-1.0, in1=turned_back[t0][:, 0:width], op0=MULT, op1=MAX
+                )
             nc.sync.dma_start(out=out[:, P * t0 : P * t1], in_=final[:, 0:width])
 
-        order = [("turn", 0, 0), ("turn", 0, 1), ("lift",), ("quantise", 0, 0)]
-        order.extend([("half", 0, 0), ("turn", 1, 0), ("half", 0, 1), ("quantise", 0, 1), ("turn", 1, 1), ("half", 0, 2), ("half", 1, 0), ("turn", 2, 0), ("half", 1, 1), ("turn", 2, 1), ("half", 1, 2)])
-        first_group = [("straight", straight_groups[0], t) for t in range(HALF_TILES, D_TILES)]
-        for j in range(1, N_BLOCKS):
-            filler = first_group[: (len(first_group) + N_BLOCKS - 1 - j) // (N_BLOCKS - j)]
-            first_group = first_group[len(filler) :]
-            if blocks[j]["negated"]:
-                order.extend([("negate", j)] + filler + [("quantise", j)])
+        order = []
+        pools = {"S": [], "P": []}
+        for token in ORDER.split():
+            if token[0] in "SP" and len(token) == 1:
+                order.append(pools[token][0])
+                pools[token] = pools[token][1:]
+            elif token[0] == "X":
+                pools["S"] = pools["S"] + [("straight", straight_groups[int(token[1])], t) for t in range(HALF_TILES if token[1] == "0" else 0, D_TILES)]
+            elif token[0] == "Y":
+                pools["P"] = pools["P"] + [("pair", pair_groups[int(token[1])], t) for t in range(D_TILES)]
+            elif token[0] == "Q":
+                order.append(("quantise",) + tuple([int(c) for c in token[1:]]))
+            elif token[0] == "H":
+                order.append(("half", int(token[1]), int(token[2])))
+            elif token[0] == "T":
+                order.append(("turn", int(token[1]), int(token[2])))
             else:
-                order.extend([("quantise", j)] + filler)
-        assert not first_group
-        straight = [("straight", g, t) for t in range(D_TILES) for g in straight_groups[1:]]
-        paired = [("pair", g, t) for t in range(D_TILES) for g in pair_groups]
-        order.extend(straight[:STRAIGHT_FIRST])
-        straight = straight[STRAIGHT_FIRST:]
+                order.append({"N": ("negate", int(token[1]) if token[0] == "N" else 0), "L": ("lift",), "B": ("bias",)}[token[0]])
+        rest = sorted(pools["S"] + pools["P"], key=lambda st: (st[2], st[1]))
+        straight = [st for st in rest if st[0] == "straight"]
+        paired = [st for st in rest if st[0] == "pair"]
         n_straight, n_paired = len(straight), len(paired)
         while straight or paired:
             if paired and (not straight or len(paired) * n_straight >= len(straight) * n_paired):
@@ -379,10 +406,6 @@ def tile_conceptembedmodel_pa_kernel(tc, x, conv_w_words, conv_w_scales, conv_b,
                 if s < n_steps:
                     write_step(order[s])
                     written.add(order[s])
-                    if order[s] == ("quantise", BIAS_AFTER):
-                        bias_turned = psum_t.tile([P, P], BF16, name="turned")
-                        nc.tensor.transpose(bias_turned[:], bias_rows[:], ident_bf[:])
-                        nc.scalar.copy(out=bias_cols[:], in_=bias_turned[:, 0:D_TILES])
                 for t in range(D_TILES):
                     if s == bias_step[t]:
                         add_bias(t)

@@ -27,12 +27,12 @@ COLS = 512
 ROWS_EACH = COLS // P
 TILES = 2
 
-PLAN = "SPPSSS"
+PLAN = "SSSSPP"
 SEQUENCES = {"S": COLS // L, "P": 2 * COLS // L}
 BLOCKS = {"S": 1, "P": 2}
 N_BLOCKS = sum([BLOCKS[kind] for kind in PLAN])
 N_PAIR_GROUPS = len([kind for kind in PLAN if kind == "P"])
-ORDER = "T00 T01 L Q00 X0 H00 T10 H01 Q01 T11 H02 H10 T20 H11 T21 H12 N1 T30 T31 S Q1 Q2 Y0 B N3 T40 T41 T50 T51 S Q3 S Q4 Y1 T60 T61 Q5 X1 S S T70 T71 Q6 X2 S S Q7 X3 S S S P S S P S P S P S P S P S S P S P S P S P S P S S P S P S P S P S P S"
+ORDER = "T00 T01 L Q00 X0 H00 T10 H01 Q01 T11 H02 H10 T20 H11 T21 H12 Q1 X1 S S T30 T31 Q2 X2 B S S T40 T41 Q3 X3 S S T50 T51 N4 S Q4 T60 T61 T70 T71 Q5 Y0 S S N6 S Q6 S Q7 Y1 S S S P S P S P S P S P S P S P S P S P S P S P S P S P S P S P S P"
 TILE_LOADS = 2
 
 HALVES = 2

@@ -40,12 +40,14 @@ HALF = COLS // HALVES
 HALF_SEQUENCES = HALF // L
 HALF_TILES = 3
 
-LEAD = {"turn": 0, "lift": 0, "bias": 0, "quantise": 0, "negate": 0, "half": 5, "straight": 2, "pair": 8}
+LEAD = {"turn": 0, "lift": 0, "bias": 0, "quantise": 0, "negate": 0, "half": 5, "straight": 2, "base": 2, "pair": 8, "join": 8}
+JOIN_TILES = 0
 STRAIGHT_FIRST = 3
 
 FINISH_GROUPS = ((0, 4), (4, 7), (7, 8))
 S_NEG = ()
 T_BANKS = (0, 2)
+TAIL_FROM = 0
 BIAS_AFTER = 2
 BIAS_LAG = 1
 BACK_LAG = 8
@@ -251,6 +253,20 @@ def tile_conceptembedmodel_pa_kernel(tc, x, conv_w_words, conv_w_scales, conv_b,
                 z = psum_v.tile([P, COLS], F32, name="z")
                 multiply(z, step[2], groups[step[1]]["blocks"][0], True, True)
                 ready[step] = z
+            elif kind == "pair" and step[2] >= D_TILES - JOIN_TILES:
+                pass
+            elif kind == "base":
+                z = psum_v.tile([P, COLS], F32, name="z")
+                multiply(z, step[2], groups[step[1]]["blocks"][1], True, True)
+                ready[step] = z
+            elif kind == "join":
+                first, second = groups[step[1]]["blocks"]
+                z_rise = psum_s.tile([P, COLS], F32, name="zs")
+                multiply(z_rise, step[2], second, True, False)
+                multiply(z_rise, step[2], first, False, True)
+                rise = rises.tile([P, COLS], F32, name="rise")
+                nc.scalar.activation(out=rise[:], in_=z_rise[:], func=RELU, scale=-1.0)
+                ready[step] = rise
             elif kind == "pair":
                 first, second = groups[step[1]]["blocks"]
                 z_first = psum_s.tile([P, COLS], F32, name="zs")
@@ -267,7 +283,13 @@ def tile_conceptembedmodel_pa_kernel(tc, x, conv_w_words, conv_w_scales, conv_b,
 
         def write_step(step):
             kind = step[0]
-            if kind in ("turn", "bias"):
+            if kind == "join":
+                total = sums.tile([P, COLS], F32, name="total")
+                nc.vector.scalar_tensor_tensor(
+                    out=total[:], in0=ready[("base", step[1], step[2])][:], scalar=bias_cols[:, step[2] : step[2] + 1], in1=ready[step][:], op0=ADD, op1=ADD
+                )
+                ready[("pair", step[1], step[2])] = total
+            elif kind in ("turn", "bias", "base"):
                 pass
             elif kind == "lift":
                 copy_out(nc.vector.tensor_copy, blocks[0], lifts[0], 0, 1, 1)
@@ -305,7 +327,7 @@ def tile_conceptembedmodel_pa_kernel(tc, x, conv_w_words, conv_w_scales, conv_b,
             return [("quantise", 0, h) for h in range(HALVES)] if j == 0 else [("quantise", j)]
 
         def codes_needed(step):
-            if step[0] in ("straight", "pair"):
+            if step[0] in ("straight", "pair", "join", "base"):
                 return [q for j in groups[step[1]]["blocks"] for q in quantises(j)]
             if step[0] == "half":
                 return [("quantise", 0, step[1])]
@@ -317,20 +339,23 @@ def tile_conceptembedmodel_pa_kernel(tc, x, conv_w_words, conv_w_scales, conv_b,
 
         def add_bias(t):
             cols = best[t][:, 0:n_straight_sequences]
-            if t == D_TILES - 1:
-                nc.vector.tensor_scalar_add(out=cols, in0=cols, scalar1=bias_cols[:, t : t + 1])
-            else:
+            if True:
                 nc.scalar.activation(out=cols, in_=cols, func=IDENTITY, bias=bias_cols[:, t : t + 1])
             shifted[t] = best[t]
 
         def turn_back(t):
             t0, t1 = [g for g in FINISH_GROUPS if g[0] <= t < g[1]][0]
             if t == t0:
-                back = psum_t.tile([P, COLS], F32, name="turned")
+                back = psum_t.tile([P, COLS], F32, name="turned") if t1 < D_TILES else psum_v.tile([P, COLS], F32, name="z")
                 turned_back[t0] = back
             back = turned_back[t0]
             nc.tensor.transpose(back[:, P * (t - t0) : P * (t - t0 + 1)], shifted[t][:], ident[:])
-            if t == t1 - 1:
+            if t == t1 - 1 and t0 == 0:
+                start_elu(t0, t1)
+
+        def start_elu(t0, t1):
+            back = turned_back[t0]
+            if True:
                 width = P * (t1 - t0)
                 grown = fin.tile([P, COLS], F32, name="grown")
                 nc.scalar.activation(out=grown[:, 0:width], in_=back[:, 0:width], func=EXP)
@@ -342,8 +367,11 @@ def tile_conceptembedmodel_pa_kernel(tc, x, conv_w_words, conv_w_scales, conv_b,
             width = P * (t1 - t0)
             final = fin.tile([P, COLS], F32, name="final")
             if t1 == D_TILES:
-                nc.vector.tensor_scalar(out=below[t0][:, 0:width], in0=below[t0][:, 0:width], scalar1=1.0, scalar2=-1.0, op0=MIN, op1=ADD)
-                nc.vector.tensor_tensor(out=final[:, 0:width], in0=below[t0][:, 0:width], in1=turned_back[t0][:, 0:width], op=MAX)
+                above = fin.tile([P, COLS], F32, name="above")
+                nc.vector.tensor_scalar_max(out=above[:, 0:width], in0=turned_back[t0][:, 0:width], scalar1=0.0)
+                nc.vector.scalar_tensor_tensor(
+                    out=final[:, 0:width], in0=below[t0][:, 0:width], scalar=-1.0, in1=above[:, 0:width], op0=ADD, op1=MIN
+                )
             else:
                 nc.vector.scalar_tensor_tensor(
                     out=final[:, 0:width], in0=below[t0][:, 0:width], scalar=-1.0, in1=turned_back[t0][:, 0:width], op0=MULT, op1=MAX
@@ -354,12 +382,14 @@ def tile_conceptembedmodel_pa_kernel(tc, x, conv_w_words, conv_w_scales, conv_b,
         pools = {"S": [], "P": []}
         for token in ORDER.split():
             if token[0] in "SP" and len(token) == 1:
-                order.append(pools[token][0])
+                order.extend(pools[token][:1])
                 pools[token] = pools[token][1:]
             elif token[0] == "X":
-                pools["S"] = pools["S"] + [("straight", straight_groups[int(token[1])], t) for t in range(HALF_TILES if token[1] == "0" else 0, D_TILES)]
+                pools["S"] = pools["S"] + [("straight", straight_groups[int(token[1])], t) for t in range(HALF_TILES if token[1] == "0" else 0, D_TILES if token[1] == "0" else D_TILES - JOIN_TILES)]
+            elif token[0] == "Z":
+                pools = {q: sorted(pools[q], key=lambda st: (st[2], st[1])) for q in pools}
             elif token[0] == "Y":
-                pools["P"] = pools["P"] + [("pair", pair_groups[int(token[1])], t) for t in range(D_TILES)]
+                pools["P"] = pools["P"] + [("pair", pair_groups[int(token[1])], t) for t in range(D_TILES - JOIN_TILES)]
             elif token[0] == "Q":
                 order.append(("quantise",) + tuple([int(c) for c in token[1:]]))
             elif token[0] == "H":
@@ -379,17 +409,26 @@ def tile_conceptembedmodel_pa_kernel(tc, x, conv_w_words, conv_w_scales, conv_b,
             else:
                 order.append(straight[0])
                 straight = straight[1:]
+        for t in range(D_TILES - JOIN_TILES, D_TILES):
+            for k in range(len(straight_groups) - 1):
+                if k < len(pair_groups):
+                    order.extend([("base", pair_groups[k], t), ("join", pair_groups[k], t)])
+                order.append(("straight", straight_groups[1 + k], t))
+            order.extend([("pair", g, t) for g in pair_groups])
         n_steps = len(order)
+        last_straight = {}
         last_reduce = {}
         for s in range(n_steps):
             if order[s][0] in ("straight", "pair"):
                 last_reduce[order[s][2]] = s
+                if order[s][0] == "straight":
+                    last_straight[order[s][2]] = s
 
-        bias_step = {t: last_reduce[t] + BIAS_LAG for t in range(D_TILES)}
+        bias_step = {t: last_straight[t] + BIAS_LAG for t in range(D_TILES)}
         back_step = {
-            t: min(last_reduce[t] + BACK_LAG, max(bias_step[t], n_steps - 1 - LEAD["straight"])) for t in range(D_TILES)
+            t: min(last_reduce[t] + BACK_LAG, max(last_reduce[t] + 1, n_steps - 1 - LEAD["straight"])) for t in range(D_TILES)
         }
-        store_step = {g: min(back_step[g[1] - 1] + STORE_LAG, n_steps) for g in FINISH_GROUPS}
+        store_step = {g: n_steps if g[1] > TAIL_FROM else min(back_step[g[1] - 1] + STORE_LAG, n_steps) for g in FINISH_GROUPS}
 
         with tc.manual_schedule():
             idle_bank = psum_v.tile([P, COLS], F32, name="z")
@@ -409,8 +448,12 @@ def tile_conceptembedmodel_pa_kernel(tc, x, conv_w_words, conv_w_scales, conv_b,
                 for t in range(D_TILES):
                     if s == bias_step[t]:
                         add_bias(t)
+                for t in range(D_TILES):
                     if s == back_step[t]:
                         turn_back(t)
+                for g in FINISH_GROUPS[1:]:
+                    if s == max(back_step[g[1] - 1], bias_step[D_TILES - 1]):
+                        start_elu(g[0], g[1])
                 for g in FINISH_GROUPS:
                     if s == store_step[g]:
                         store(g[0], g[1])

@@ -32,7 +32,7 @@ SEQUENCES = {"S": COLS // L, "P": 2 * COLS // L}
 BLOCKS = {"S": 1, "P": 2}
 N_BLOCKS = sum([BLOCKS[kind] for kind in PLAN])
 N_PAIR_GROUPS = len([kind for kind in PLAN if kind == "P"])
-ORDER = "T00 T01 L Q00 X0 H00 T10 H01 Q01 T11 H02 H10 T20 H11 T21 H12 Q1 X1 S S T30 T31 Q2 X2 B S S T40 T41 Q3 X3 S S T50 T51 N4 S Q4 T60 T61 T70 T71 Q5 Y0 S S N6 S Q6 S Q7 Y1 S S S P S P S P S P S P S P S P S P S P S P S P S P S P S P S P S P"
+ORDER = "T00 T01 L Q00 X0 H00 T10 H01 Q01 T11 H02 H10 T20 H11 T21 H12 Q1 X1 S S T30 T31 Q2 X2 B S S T40 T41 Q3 X3 S T50 T51 N4 S Q4 T60 T61 T70 T71 Q5 Y0 N6 Q6 Q7 Y1 S S S S S P S P S P S S P S P S P S S P S P S P S S P S P S P S S P S P S P P"
 TILE_LOADS = 2
 
 HALVES = 2

from contextlib import ExitStack

import concourse.mybir as mybir
from concourse.masks import make_identity

BF16 = mybir.dt.bfloat16
F32 = mybir.dt.float32
I32 = mybir.dt.int32
U32 = mybir.dt.uint32
U8 = mybir.dt.uint8
FP8X4 = mybir.dt.float8_e4m3fn_x4
FP4X4 = mybir.dt.float4_e2m1fn_x4
EXP = mybir.ActivationFunctionType.Exp
RELU = mybir.ActivationFunctionType.Relu
IDENTITY = mybir.ActivationFunctionType.Identity
MULT = mybir.AluOpType.mult
MIN = mybir.AluOpType.min
ADD = mybir.AluOpType.add
MAX = mybir.AluOpType.max

P = 128
B, L, F, D = 128, 32, 512, 1024
PACK = 4
WORDS = F // 2
D_TILES = D // P
COLS = 512
ROWS_EACH = COLS // P
TILES = 2

PLAN = "SSSSPP"
SEQUENCES = {"S": COLS // L, "P": 2 * COLS // L}
BLOCKS = {"S": 1, "P": 2}
N_BLOCKS = sum([BLOCKS[kind] for kind in PLAN])
N_PAIR_GROUPS = len([kind for kind in PLAN if kind == "P"])
ORDER = "T00 T01 L Q00 X0 H00 T10 H01 Q01 T11 H02 H10 T20 H11 T21 H12 Q1 X1 S S T30 T31 Q2 X2 B S S T40 T41 Q3 X3 S T50 T51 N4 S Q4 T60 T61 T70 T71 Q5 Y0 N6 Q6 Q7 Y1 S S S S S P S P S P S S P S P S P S S P S P S P S S P S P S P S S P S P S P P"
TILE_LOADS = 2

HALVES = 2
HALF = COLS // HALVES
HALF_SEQUENCES = HALF // L
HALF_TILES = 3

LEAD = {"turn": 0, "lift": 0, "bias": 0, "quantise": 0, "negate": 0, "half": 5, "straight": 2, "base": 2, "pair": 8, "join": 8}
JOIN_TILES = 0
STRAIGHT_FIRST = 3

FINISH_GROUPS = ((0, 4), (4, 7), (7, 8))
S_NEG = ()
T_BANKS = (0, 2)
TAIL_FROM = 0
BIAS_AFTER = 2
BIAS_LAG = 1
BACK_LAG = 8
STORE_LAG = 6

FLOPS = 2 * B * L * F * D


def tile_conceptembedmodel_pa_kernel(tc, x, conv_w_words, conv_w_scales, conv_b, out):
    nc = tc.nc
    with ExitStack() as ctx:
        const = ctx.enter_context(tc.tile_pool(name="const", bufs=1))
        x_pool = ctx.enter_context(tc.tile_pool(name="x_pool", bufs=TILES * TILE_LOADS))
        x_big = ctx.enter_context(tc.tile_pool(name="x_big", bufs=N_BLOCKS - TILE_LOADS))
        stage = ctx.enter_context(tc.tile_pool(name="stage", bufs=N_BLOCKS))
        minus_pool = ctx.enter_context(tc.tile_pool(name="minus_pool", bufs=N_PAIR_GROUPS))
        keep = ctx.enter_context(tc.tile_pool(name="keep", bufs=N_BLOCKS))
        sums = ctx.enter_context(tc.tile_pool(name="sums", bufs=LEAD["pair"]))
        rises = ctx.enter_context(tc.tile_pool(name="rises", bufs=6))
        fin = ctx.enter_context(tc.tile_pool(name="fin", bufs=len(FINISH_GROUPS)))
        psum_t = ctx.enter_context(tc.psum_pool(name="psum_t", bufs=2))
        psum_v = ctx.enter_context(tc.psum_pool(name="psum_v", bufs=3))
        psum_s = ctx.enter_context(tc.psum_pool(name="psum_s", bufs=3))

        w_scales = const.tile([P, D], U8, align_bytes=64)
        nc.vector.memset(w_scales[:].bitcast(I32), 0)
        zero_col = const.tile([P, 1], F32)
        nc.vector.memset(zero_col[:], 0.0)
        one_col = const.tile([P, 1], F32)
        nc.scalar.activation(out=one_col[:], in_=zero_col[:], func=EXP)
        ident = const.tile([P, P], F32)
        make_identity(nc, ident[:])
        ident_bf = const.tile([P, P], BF16)
        make_identity(nc, ident_bf[:])
        bias_rows = const.tile([P, P], BF16)
        nc.gpsimd.memset(bias_rows[:], 0.0)

        zeros = const.tile([P, COLS], BF16)
        nc.vector.memset(zeros[:], 0.0)

        rows = x.rearrange("b l f -> (b l) f")
        first_sequence = {"S": 0, "P": SEQUENCES["S"] * len([kind for kind in PLAN if kind == "S"])}
        n_straight_sequences = first_sequence["P"]
        groups = []
        blocks = []
        for kind in PLAN:
            b0 = first_sequence[kind]
            view = rows[L * b0 : L * (b0 + SEQUENCES[kind]), :].rearrange("(p n) f -> p (n f)", n=ROWS_EACH * BLOCKS[kind])
            group = {"kind": kind, "b0": b0, "width": SEQUENCES[kind], "blocks": []}
            for a in range(BLOCKS[kind]):
                group["blocks"].append(len(blocks))
                tile_run = ROWS_EACH * F // TILES
                tile_views = [view[:, ROWS_EACH * F * a + tile_run * k : ROWS_EACH * F * a + tile_run * (k + 1)] for k in range(TILES)]
                if not blocks:
                    tile_views = [rows[HALF * h : HALF * (h + 1), :].rearrange("(p n) f -> p (n f)", n=ROWS_EACH // HALVES) for h in range(HALVES)]
                blocks.append({
                    "index": len(blocks),
                    "view": view[:, ROWS_EACH * F * a : ROWS_EACH * F * (a + 1)],
                    "tile_views": tile_views,
                    "negated": kind == "P" and a == 0,
                })
            groups.append(group)
            first_sequence[kind] += SEQUENCES[kind]
        assert first_sequence["P"] == B
        straight_groups = [g for g in range(len(groups)) if groups[g]["kind"] == "S"]
        pair_groups = [g for g in range(len(groups)) if groups[g]["kind"] == "P"]

        tile_width = ROWS_EACH * F // TILES

        def load_by_tiles(block):
            block["x"] = []
            for k in range(TILES):
                x_tile = x_pool.tile([P, tile_width], BF16, name="x_tile")
                nc.sync.dma_start(out=x_tile[:], in_=block["tile_views"][k])
                block["x"].append(x_tile[:, :])

        load_by_tiles(blocks[0])
        scale_rows = conv_w_scales.rearrange("g q n -> (g q) n")
        for quadrant in range(4):
            nc.sync.dma_start(
                out=w_scales[32 * quadrant : 32 * quadrant + 4, :].bitcast(I32),
                in_=scale_rows[4 * quadrant : 4 * quadrant + 4, :].bitcast(I32),
            )
        w_words = const.tile([P, 2 * D], U8, align_bytes=64)
        nc.sync.dma_start(
            out=w_words[:].bitcast(I32),
            in_=conv_w_words.rearrange("g p n -> (g p) n").bitcast(I32),
        )
        for j in range(1, N_BLOCKS):
            if j == N_BLOCKS // 2:
                nc.sync.dma_start(out=bias_rows[0:D_TILES, :], in_=conv_b.rearrange("(t p) -> t p", p=P))
            if j < TILE_LOADS:
                load_by_tiles(blocks[j])
            else:
                x_block = x_big.tile([P, TILES * tile_width], BF16, name="x_block")
                nc.sync.dma_start(out=x_block[:], in_=blocks[j]["view"])
                blocks[j]["x"] = [x_block[:, tile_width * k : tile_width * (k + 1)] for k in range(TILES)]

        best = [const.tile([P, B], F32, name="best%d" % t) for t in range(D_TILES)]
        bias_cols = const.tile([P, D_TILES], F32)

        def copy_out(engine_copy, block, turned, k, i0, n):
            width = PACK * P
            first = 2 * k + i0
            if block["negated"] and block["index"] in S_NEG:
                nc.scalar.activation(
                    out=block["grouped"][:, width * first : width * (first + n)].rearrange("p (c u e) -> p c u e", u=2, e=2),
                    in_=turned[:].rearrange("p u i c -> p u (i c)").bitcast(BF16).rearrange("p u (c e) -> p c u e", e=2),
                    func=IDENTITY,
                    scale=-1.0,
                )
                return
            engine_copy(
                out=block["grouped"][:, width * first : width * (first + n)].bitcast(F32).rearrange("p (c u) -> p c u", u=2),
                in_=turned[:].rearrange("p u i c -> p (i c) u"),
            )

        def turn_rows(j, k, i0, n):
            block = blocks[j]
            if "grouped" not in block:
                grouped = stage.tile([P, COLS * PACK], BF16, align_bytes=64, name="grouped")
                block["grouped"] = grouped
            x_words = block["x"][k].bitcast(F32)
            if len(turns) % 5 in T_BANKS:
                turned = psum_t.tile([P, 2, n, P], F32, name="turned")
            else:
                turned = psum_s.tile([P, 2, n, P], F32, name="zs")
            turns.append(turned)
            for i in range(n):
                for u in range(2):
                    nc.tensor.transpose(
                        turned[:, u, i, :],
                        x_words[:, WORDS * (i0 + i) + u : WORDS * (i0 + i + 1) : 2],
                        ident[:],
                    )
            return turned

        turns = []
        lifts = []

        def turn(j, k):
            block = blocks[j]
            if k in block.get("done", []):
                return
            block.setdefault("done", []).append(k)
            if (j, k) == (0, 0):
                copy_out(nc.scalar.copy, block, turn_rows(0, 0, 0, 1), 0, 0, 1)
                lifts.append(turn_rows(0, 0, 1, 1))
            else:
                copy_out(nc.scalar.copy, block, turn_rows(j, k, 0, 2), k, 0, 2)

        def transpose_block(j):
            for k in range(TILES):
                if k not in blocks[j].get("done", []):
                    turn(j, k)

        def negate_block(j):
            block = blocks[j]
            minus = minus_pool.tile([P, COLS * PACK], BF16, align_bytes=64, name="minus")
            nc.vector.tensor_scalar_mul(out=minus[:], in0=block["grouped"][:], scalar1=-1.0)
            block["grouped"] = minus

        def quantise_cols(j, c0, c1):
            block = blocks[j]
            if "codes" not in block:
                codes = keep.tile([P, COLS], U32, align_bytes=64, name="codes")
                scales = keep.tile([P, COLS], U8, align_bytes=64, name="scales")
                block["codes"] = (codes, scales)
            codes, scales = block["codes"]
            nc.vector.quantize_mx(
                out=codes[:, c0:c1].bitcast(FP8X4), scales=scales[:, c0:c1], in_=block["grouped"][:, PACK * c0 : PACK * c1]
            )

        def multiply(bank, t, j, start, stop, c0=0, c1=COLS):
            codes, scales = blocks[j]["codes"]
            nc.tensor.matmul_mx(
                out=bank[:, 0 : c1 - c0],
                lhsT=w_words[:, 2 * P * t : 2 * P * (t + 1)].bitcast(FP4X4),
                lhsT_scale=w_scales[:, P * t : P * (t + 1)],
                rhs=codes[:, c0:c1].bitcast(FP8X4),
                rhs_scale=scales[:, c0:c1],
                start=start,
                stop=stop,
            )

        ready = {}

        def write_producers(step):
            kind = step[0]
            if kind == "turn":
                turn(step[1], step[2])
            elif kind == "bias":
                bias_turned = psum_t.tile([P, P], BF16, name="turned")
                nc.tensor.transpose(bias_turned[:], bias_rows[:], ident_bf[:])
                nc.scalar.copy(out=bias_cols[:], in_=bias_turned[:, 0:D_TILES])
            elif kind in ("negate", "quantise"):
                assert len(blocks[step[1]]["x"]) == len(blocks[step[1]]["done"])
            elif kind == "half":
                z = psum_v.tile([P, COLS], F32, name="z")
                multiply(z, step[2], 0, True, True, HALF * step[1], HALF * (step[1] + 1))
                ready[step] = z
            elif kind == "straight":
                z = psum_v.tile([P, COLS], F32, name="z")
                multiply(z, step[2], groups[step[1]]["blocks"][0], True, True)
                ready[step] = z
            elif kind == "pair" and step[2] >= D_TILES - JOIN_TILES:
                pass
            elif kind == "base":
                z = psum_v.tile([P, COLS], F32, name="z")
                multiply(z, step[2], groups[step[1]]["blocks"][1], True, True)
                ready[step] = z
            elif kind == "join":
                first, second = groups[step[1]]["blocks"]
                z_rise = psum_s.tile([P, COLS], F32, name="zs")
                multiply(z_rise, step[2], second, True, False)
                multiply(z_rise, step[2], first, False, True)
                rise = rises.tile([P, COLS], F32, name="rise")
                nc.scalar.activation(out=rise[:], in_=z_rise[:], func=RELU, scale=-1.0)
                ready[step] = rise
            elif kind == "pair":
                first, second = groups[step[1]]["blocks"]
                z_first = psum_s.tile([P, COLS], F32, name="zs")
                multiply(z_first, step[2], first, True, True)
                z_rise = psum_s.tile([P, COLS], F32, name="zs")
                multiply(z_rise, step[2], second, True, False)
                multiply(z_rise, step[2], first, False, True)
                total = sums.tile([P, COLS], F32, name="total")
                nc.scalar.activation(out=total[:], in_=z_first[:], func=IDENTITY, scale=-1.0, bias=bias_cols[:, step[2] : step[2] + 1])
                rise = rises.tile([P, COLS], F32, name="rise")
                nc.scalar.activation(out=rise[:], in_=z_rise[:], func=RELU)
                nc.gpsimd.tensor_add(out=total[:], in0=rise[:], in1=total[:])
                ready[step] = total

        def write_step(step):
            kind = step[0]
            if kind == "join":
                total = sums.tile([P, COLS], F32, name="total")
                nc.vector.scalar_tensor_tensor(
                    out=total[:], in0=ready[("base", step[1], step[2])][:], scalar=bias_cols[:, step[2] : step[2] + 1], in1=ready[step][:], op0=ADD, op1=ADD
                )
                ready[("pair", step[1], step[2])] = total
            elif kind in ("turn", "bias", "base"):
                pass
            elif kind == "lift":
                copy_out(nc.vector.tensor_copy, blocks[0], lifts[0], 0, 1, 1)
            elif kind == "quantise" and step[1] == 0:
                quantise_cols(0, HALF * step[2], HALF * (step[2] + 1))
            elif kind == "quantise":
                quantise_cols(step[1], 0, COLS)
            elif kind == "half":
                h = step[1]
                nc.vector.tensor_reduce(
                    out=best[step[2]][:, HALF_SEQUENCES * h : HALF_SEQUENCES * (h + 1)],
                    in_=ready[step][:, 0:HALF].rearrange("p (i c q) -> p c i q", i=2, c=HALF_SEQUENCES),
                    axis=mybir.AxisListType.XY,
                    op=MAX,
                )
            elif kind == "straight" and step[1] == 0:
                nc.vector.tensor_reduce(
                    out=best[step[2]][:, 0 : SEQUENCES["S"]].rearrange("p (h c) -> p h c", h=HALVES),
                    in_=ready[step][:].rearrange("p (h i c q) -> p h c i q", h=HALVES, i=2, c=HALF_SEQUENCES),
                    axis=mybir.AxisListType.XY,
                    op=MAX,
                )
            elif kind == "negate":
                negate_block(step[1])
            else:
                group = groups[step[1]]
                nc.vector.tensor_reduce(
                    out=best[step[2]][:, group["b0"] : group["b0"] + group["width"]],
                    in_=ready[step][:].rearrange("p (i c q) -> p c i q", i=ROWS_EACH, c=group["width"]),
                    axis=mybir.AxisListType.XY,
                    op=MAX,
                )

        def quantises(j):
            return [("quantise", 0, h) for h in range(HALVES)] if j == 0 else [("quantise", j)]

        def codes_needed(step):
            if step[0] in ("straight", "pair", "join", "base"):
                return [q for j in groups[step[1]]["blocks"] for q in quantises(j)]
            if step[0] == "half":
                return [("quantise", 0, step[1])]
            return []

        shifted = {}
        turned_back = {}
        below = {}

        def add_bias(t):
            cols = best[t][:, 0:n_straight_sequences]
            if True:
                nc.scalar.activation(out=cols, in_=cols, func=IDENTITY, bias=bias_cols[:, t : t + 1])
            shifted[t] = best[t]

        def turn_back(t):
            t0, t1 = [g for g in FINISH_GROUPS if g[0] <= t < g[1]][0]
            if t == t0:
                back = psum_t.tile([P, COLS], F32, name="turned") if t1 < D_TILES else psum_v.tile([P, COLS], F32, name="z")
                turned_back[t0] = back
            back = turned_back[t0]
            nc.tensor.transpose(back[:, P * (t - t0) : P * (t - t0 + 1)], shifted[t][:], ident[:])
            if t == t1 - 1 and t0 == 0:
                start_elu(t0, t1)

        def start_elu(t0, t1):
            back = turned_back[t0]
            if True:
                width = P * (t1 - t0)
                grown = fin.tile([P, COLS], F32, name="grown")
                nc.scalar.activation(out=grown[:, 0:width], in_=back[:, 0:width], func=EXP)
                if t1 < D_TILES:
                    nc.scalar.activation(out=grown[:, 0:width], in_=grown[:, 0:width], func=RELU, bias=1.0, scale=-1.0)
                below[t0] = grown

        def store(t0, t1):
            width = P * (t1 - t0)
            final = fin.tile([P, COLS], F32, name="final")
            if t1 == D_TILES:
                above = fin.tile([P, COLS], F32, name="above")
                nc.vector.tensor_scalar_max(out=above[:, 0:width], in0=turned_back[t0][:, 0:width], scalar1=0.0)
                nc.vector.scalar_tensor_tensor(
                    out=final[:, 0:width], in0=below[t0][:, 0:width], scalar=-1.0, in1=above[:, 0:width], op0=ADD, op1=MIN
                )
            else:
                nc.vector.scalar_tensor_tensor(
                    out=final[:, 0:width], in0=below[t0][:, 0:width], scalar=-1.0, in1=turned_back[t0][:, 0:width], op0=MULT, op1=MAX
                )
            nc.sync.dma_start(out=out[:, P * t0 : P * t1], in_=final[:, 0:width])

        order = []
        pools = {"S": [], "P": []}
        for token in ORDER.split():
            if token[0] in "SP" and len(token) == 1:
                order.extend(pools[token][:1])
                pools[token] = pools[token][1:]
            elif token[0] == "X":
                pools["S"] = pools["S"] + [("straight", straight_groups[int(token[1])], t) for t in range(HALF_TILES if token[1] == "0" else 0, D_TILES if token[1] == "0" else D_TILES - JOIN_TILES)]
            elif token[0] == "Z":
                pools = {q: sorted(pools[q], key=lambda st: (st[2], st[1])) for q in pools}
            elif token[0] == "Y":
                pools["P"] = pools["P"] + [("pair", pair_groups[int(token[1])], t) for t in range(D_TILES - JOIN_TILES)]
            elif token[0] == "Q":
                order.append(("quantise",) + tuple([int(c) for c in token[1:]]))
            elif token[0] == "H":
                order.append(("half", int(token[1]), int(token[2])))
            elif token[0] == "T":
                order.append(("turn", int(token[1]), int(token[2])))
            else:
                order.append({"N": ("negate", int(token[1]) if token[0] == "N" else 0), "L": ("lift",), "B": ("bias",)}[token[0]])
        rest = sorted(pools["S"] + pools["P"], key=lambda st: (st[2], st[1]))
        straight = [st for st in rest if st[0] == "straight"]
        paired = [st for st in rest if st[0] == "pair"]
        n_straight, n_paired = len(straight), len(paired)
        while straight or paired:
            if paired and (not straight or len(paired) * n_straight >= len(straight) * n_paired):
                order.append(paired[0])
                paired = paired[1:]
            else:
                order.append(straight[0])
                straight = straight[1:]
        for t in range(D_TILES - JOIN_TILES, D_TILES):
            for k in range(len(straight_groups) - 1):
                if k < len(pair_groups):
                    order.extend([("base", pair_groups[k], t), ("join", pair_groups[k], t)])
                order.append(("straight", straight_groups[1 + k], t))
            order.extend([("pair", g, t) for g in pair_groups])
        n_steps = len(order)
        last_straight = {}
        last_reduce = {}
        for s in range(n_steps):
            if order[s][0] in ("straight", "pair"):
                last_reduce[order[s][2]] = s
                if order[s][0] == "straight":
                    last_straight[order[s][2]] = s

        bias_step = {t: last_straight[t] + BIAS_LAG for t in range(D_TILES)}
        back_step = {
            t: min(last_reduce[t] + BACK_LAG, max(last_reduce[t] + 1, n_steps - 1 - LEAD["straight"])) for t in range(D_TILES)
        }
        store_step = {g: n_steps if g[1] > TAIL_FROM else min(back_step[g[1] - 1] + STORE_LAG, n_steps) for g in FINISH_GROUPS}

        with tc.manual_schedule():
            idle_bank = psum_v.tile([P, COLS], F32, name="z")
            for warm_up in range(4):
                nc.tensor.matmul(out=idle_bank[:], lhsT=zeros[:, 0:P], rhs=zeros[:], start=True, stop=True)
            produced = set()
            written = set()
            for s in range(n_steps + 1):
                for ahead in range(s, min(n_steps, s + max(LEAD.values()) + 1)):
                    step = order[ahead]
                    if step not in produced and ahead - LEAD[step[0]] <= s and all(q in written for q in codes_needed(step)):
                        write_producers(step)
                        produced.add(step)
                if s < n_steps:
                    write_step(order[s])
                    written.add(order[s])
                for t in range(D_TILES):
                    if s == bias_step[t]:
                        add_bias(t)
                for t in range(D_TILES):
                    if s == back_step[t]:
                        turn_back(t)
                for g in FINISH_GROUPS[1:]:
                    if s == max(back_step[g[1] - 1], bias_step[D_TILES - 1]):
                        start_elu(g[0], g[1])
                for g in FINISH_GROUPS:
                    if s == store_step[g]:
                        store(g[0], g[1])
